import numpy as np
import ml_dtypes


def mxq(x, axis, fmt="e4m3"):
    dtype, down = {"e4m3": (ml_dtypes.float8_e4m3fn, 7), "e5m2": (ml_dtypes.float8_e5m2, 14)}[fmt]
    v = np.moveaxis(np.asarray(x, np.float32).astype(ml_dtypes.bfloat16).astype(np.float64), axis, -1)
    blocks = v.reshape(v.shape[:-1] + (-1, 32))
    amax = np.abs(blocks).max(-1, keepdims=True)
    byte = np.maximum(np.where(amax > 0, np.frexp(amax)[1] - 1 + 127, 0) - down, 1)
    scale = np.exp2(byte - 127.0)
    codes = (blocks / scale).astype(np.float32).astype(dtype).astype(np.float64)
    return np.moveaxis((codes * scale).reshape(v.shape), -1, axis)


WIDE = False


def mx_kscale(k):
    if not WIDE:
        return np.ones(k)
    levels = np.array([10, -10, 5, -5, 0])
    if k % 512:
        return np.exp2(np.random.permutation(np.resize(levels, k // 32))).repeat(32)
    a = np.empty((k // 512, 16))
    for p in range(k // 512):
        a[p, :8] = np.random.permutation(np.resize(levels, 8))
        for g in range(8):
            far = levels[np.abs(levels - a[p, g]) >= 10]
            a[p, g + 8] = far[np.random.randint(len(far))]
    return np.exp2(a.ravel()).repeat(32)


BF16 = ml_dtypes.bfloat16


def bf(x):
    return np.asarray(x, np.float32).astype(BF16)


def f64(x):
    return np.asarray(x).astype(np.float64)


B, N, D, HEAD, HALF = 1, 1024, 512, 1024, 512
E = HEAD + HALF + HALF
EPS_RMS = 1e-6
EPS_NORM = 1e-12


def setup_inputs():
    s = mx_kscale(D)
    return {"x": bf(np.random.standard_normal((B, N, D))),
            "g": bf((1.0 + 0.1 * np.random.standard_normal(D)) * s),
            "W1": bf(np.random.standard_normal((D, E)) / np.sqrt(D) / s[:, None]),
            "b1": bf(np.random.standard_normal(E) * 0.3)}


def reference(x, g, W1, b1):
    x = f64(x)
    xn = x * (1.0 / np.sqrt(np.mean(np.square(x), axis=-1, keepdims=True) + EPS_RMS)) * f64(g)
    pre = (mxq(xn, 2, "e4m3") @ mxq(f64(W1), 0, "e4m3")) + f64(b1)
    enriched = np.square(np.maximum(pre, 0.0))
    head = enriched[..., :HEAD]
    x_left = enriched[..., HEAD:HEAD + HALF]
    x_right = enriched[..., HEAD + HALF:]
    nrm = np.sqrt(np.sum(np.square(x_right), axis=-1, keepdims=True))
    xr_n = x_right / np.maximum(nrm, EPS_NORM)
    return head, x_left, xr_n

@@ -1,0 +1,201 @@
+from contextlib import ExitStack
+
+import concourse.masks as masks
+import concourse.mybir as mybir
+
+F32 = mybir.dt.float32
+BF16 = mybir.dt.bfloat16
+U32 = mybir.dt.uint32
+U8 = mybir.dt.uint8
+FP8X4 = mybir.dt.float8_e4m3fn_x4
+ACT = mybir.ActivationFunctionType
+ALU = mybir.AluOpType
+
+P = 128
+PACK = 4
+TOKENS = 1024
+D = 512
+HEAD = 1024
+HALF = 512
+E = HEAD + HALF + HALF
+BANK = 512
+TOK_TILES = TOKENS // P
+PAIRS = TOK_TILES // 2
+EPS_RMS = 1e-6
+EPS_NORM = 1e-12
+FLT_MAX = 3.4028234663852886e38
+
+FLOPS = 2 * TOKENS * D * E
+
+
+def tile_avey_pa_kernel(tc, x, g, W1, b1, out_0, out_1, out_2):
+    nc = tc.nc
+
+    x_rows = x.flatten_outer_dims().rearrange("(p i) k -> p i k", i=TOK_TILES)
+    head_rows = out_0.flatten_outer_dims().rearrange("(p i) f -> p i f", i=TOK_TILES)
+    left_rows = out_1.flatten_outer_dims().rearrange("(p i) f -> p i f", i=TOK_TILES)
+    right_rows = out_2.flatten_outer_dims().rearrange("(p i) f -> p i f", i=TOK_TILES)
+    w_rows = W1.rearrange("(p t) f -> p t f", t=PACK)
+
+    pieces = (
+        (right_rows, HEAD + HALF, HALF),
+        (left_rows, HEAD, HALF),
+        (head_rows, 0, HEAD),
+    )
+    bank_order = [first // BANK + b for (rows, first, width) in pieces for b in range(width // BANK)]
+
+    with ExitStack() as ctx:
+        keep = ctx.enter_context(tc.tile_pool(name="keep", bufs=1))
+        stage = ctx.enter_context(tc.tile_pool(name="stage", bufs=2))
+        flow = ctx.enter_context(tc.tile_pool(name="flow", bufs=3))
+        psum_gain = ctx.enter_context(tc.psum_pool(name="psum_gain", bufs=1))
+        psum_turn = ctx.enter_context(tc.psum_pool(name="psum_turn", bufs=2))
+        psum_acc = ctx.enter_context(tc.psum_pool(name="psum_acc", bufs=5))
+
+        warm = keep.tile([P, 1], F32)
+        nc.vector.memset(warm[:], 1.0)
+        nc.scalar.activation(out=warm[:], in_=warm[:], func=ACT.Sqrt)
+
+        ident_f32 = keep.tile([P, P], F32)
+        masks.make_identity(nc, ident_f32[:])
+        ones = keep.tile([P, P], BF16)
+        nc.vector.memset(ones[:], 1.0)
+
+        g_row = keep.tile([P, D], BF16)
+        nc.vector.memset(g_row[:], 0.0)
+        nc.scalar.dma_start(out=g_row[0:1, :], in_=g.unsqueeze(0))
+        b_row = keep.tile([P, E], BF16)
+        nc.vector.memset(b_row[:], 0.0)
+        nc.scalar.dma_start(out=b_row[0:1, :], in_=b1.unsqueeze(0))
+
+        x_sb = keep.tile([P, TOK_TILES, D], BF16)
+        for j in range(PAIRS):
+            nc.sync.dma_start(out=x_sb[:, 2 * j : 2 * j + 2, :], in_=x_rows[:, 2 * j : 2 * j + 2, :])
+        w_raw = keep.tile([P, PACK, E], BF16)
+        for b in bank_order:
+            cols = slice(b * BANK, (b + 1) * BANK)
+            nc.sync.dma_start(out=w_raw[:, :, cols], in_=w_rows[:, :, cols])
+
+        gain = psum_gain.tile([P, D], F32)
+        nc.tensor.matmul(out=gain[:], lhsT=ones[:], rhs=g_row[:], start=True, stop=True)
+        bias = keep.tile([P, E], F32)
+        for b in bank_order:
+            cols = slice(b * BANK, (b + 1) * BANK)
+            acc = psum_acc.tile([P, BANK], F32, tag="acc")
+            nc.tensor.matmul(out=acc[:], lhsT=ones[:], rhs=b_row[:, cols], start=True, stop=True)
+            nc.vector.tensor_copy(out=bias[:, cols], in_=acc[:])
+
+        x_codes = keep.tile([P, TOKENS], U32, align_bytes=64)
+        x_scales = keep.tile([P, TOKENS], U8, align_bytes=64)
+        w_codes = keep.tile([P, E], U32, align_bytes=64)
+        w_scales = keep.tile([P, E], U8, align_bytes=64)
+
+        squares = keep.tile([P, TOK_TILES, D], BF16)
+        sumsq = keep.tile([P, TOK_TILES], F32)
+        rms = keep.tile([P, TOK_TILES], F32)
+        rstd = keep.tile([P, TOK_TILES], F32)
+
+        def normalise_pair(j):
+            pair = slice(2 * j, 2 * j + 2)
+            for i in (2 * j, 2 * j + 1):
+                nc.scalar.activation(
+                    out=squares[:, i, :], in_=x_sb[:, i, :], func=ACT.Square, accum_out=sumsq[:, i : i + 1]
+                )
+            nc.scalar.activation(out=rms[:, pair], in_=sumsq[:, pair], func=ACT.Sqrt, bias=EPS_RMS, scale=1.0 / D)
+            nc.vector.reciprocal(out=rstd[:, pair], in_=rms[:, pair])
+            xn = stage.tile([P, 2, D], BF16)
+            for h in range(2):
+                i = 2 * j + h
+                nc.vector.scalar_tensor_tensor(
+                    out=xn[:, h, :],
+                    in0=x_sb[:, i, :],
+                    scalar=rstd[:, i : i + 1],
+                    in1=gain[:],
+                    op0=ALU.mult,
+                    op1=ALU.mult,
+                )
+            words = xn[:].bitcast(F32)
+            turned = psum_turn.tile([P, 2, 2, P], F32)
+            for h in range(2):
+                for u in range(2):
+                    nc.tensor.transpose(turned[:, h, u, :], words[:, h, u::2], ident_f32[:])
+            x_grouped = stage.tile([P, 2, P, PACK], BF16, align_bytes=64)
+            nc.scalar.copy(out=x_grouped[:].bitcast(F32), in_=turned[:].rearrange("p h u r -> p h r u"))
+            toks = slice(2 * j * P, (2 * j + 2) * P)
+            nc.vector.quantize_mx(
+                out=x_codes[:, toks].bitcast(FP8X4),
+                scales=x_scales[:, toks],
+                in_=x_grouped[:].rearrange("p h r t -> p (h r t)"),
+            )
+
+        def quantise_w_bank(b):
+            cols = slice(b * BANK, (b + 1) * BANK)
+            w_grouped = stage.tile([P, BANK, PACK], BF16, align_bytes=64)
+            nc.vector.tensor_copy(
+                out=w_grouped[:].rearrange("p (c i) t -> p c t i", i=4),
+                in_=w_raw[:, :, cols].rearrange("p t (c i) -> p c t i", i=4),
+            )
+            nc.vector.quantize_mx(
+                out=w_codes[:, cols].bitcast(FP8X4),
+                scales=w_scales[:, cols],
+                in_=w_grouped[:].rearrange("p f t -> p (f t)"),
+            )
+
+        norm2 = keep.tile([P, TOK_TILES], F32)
+        norm2_floor = keep.tile([P, TOK_TILES], F32)
+        norm = keep.tile([P, TOK_TILES], F32)
+        inv_norm = keep.tile([P, TOK_TILES], F32)
+
+        def enrich_tile(i):
+            toks = slice(i * P, (i + 1) * P)
+            one = slice(i, i + 1)
+            pre = flow.tile([P, E], F32)
+            enriched = flow.tile([P, E], F32)
+            for rows, first, width in pieces:
+                span = slice(first, first + width)
+                for b in range(first // BANK, (first + width) // BANK):
+                    cols = slice(b * BANK, (b + 1) * BANK)
+                    acc = psum_acc.tile([P, BANK], F32, tag="acc")
+                    nc.tensor.matmul_mx(
+                        out=acc[:],
+                        lhsT=x_codes[:, toks].bitcast(FP8X4),
+                        lhsT_scale=x_scales[:, toks],
+                        rhs=w_codes[:, cols].bitcast(FP8X4),
+                        rhs_scale=w_scales[:, cols],
+                        start=True,
+                        stop=True,
+                    )
+                    nc.vector.tensor_tensor(out=pre[:, cols], in0=acc[:], in1=bias[:, cols], op=ALU.add)
+                nc.gpsimd.tensor_scalar(
+                    out=pre[:, span], in0=pre[:, span], scalar1=FLT_MAX, scalar2=0.0, op0=ALU.min, op1=ALU.max
+                )
+                nc.scalar.activation(out=enriched[:, span], in_=pre[:, span], func=ACT.Square)
+                if rows is right_rows:
+                    fourth = flow.tile([P, HALF], BF16)
+                    nc.scalar.activation(
+                        out=fourth[:], in_=enriched[:, span], func=ACT.Square, accum_out=norm2[:, one]
+                    )
+                    nc.vector.tensor_scalar_max(out=norm2_floor[:, one], in0=norm2[:, one], scalar1=EPS_NORM * EPS_NORM)
+                    nc.scalar.activation(out=norm[:, one], in_=norm2_floor[:, one], func=ACT.Sqrt)
+                    nc.vector.reciprocal(out=inv_norm[:, one], in_=norm[:, one])
+                    unit = flow.tile([P, HALF], F32)
+                    nc.gpsimd.tensor_scalar(
+                        out=unit[:],
+                        in0=enriched[:, span],
+                        scalar1=inv_norm[:, one],
+                        scalar2=1.0,
+                        op0=ALU.mult,
+                        op1=ALU.mult,
+                    )
+                    nc.sync.dma_start(out=rows[:, i, :], in_=unit[:])
+                else:
+                    nc.sync.dma_start(out=rows[:, i, :], in_=enriched[:, span])
+
+        normalise_pair(0)
+        for b in bank_order:
+            quantise_w_bank(b)
+        for j in range(PAIRS):
+            if j + 1 < PAIRS:
+                normalise_pair(j + 1)
+            enrich_tile(2 * j)
+            enrich_tile(2 * j + 1)

@@ -21,6 +21,11 @@ E = HEAD + HALF + HALF
 BANK = 512
 TOK_TILES = TOKENS // P
 PAIRS = TOK_TILES // 2
+QUAD = 4
+GROUPS = BANK // P
+LEAD = 3
+BANKS = E // BANK
+GAIN_ROW = BANKS
 EPS_RMS = 1e-6
 EPS_NORM = 1e-12
 FLT_MAX = 3.4028234663852886e38
@@ -37,53 +42,68 @@ def tile_avey_pa_kernel(tc, x, g, W1, b1, out_0, out_1, out_2):
     right_rows = out_2.flatten_outer_dims().rearrange("(p i) f -> p i f", i=TOK_TILES)
     w_rows = W1.rearrange("(p t) f -> p t f", t=PACK)
 
-    pieces = (
-        (right_rows, HEAD + HALF, HALF),
-        (left_rows, HEAD, HALF),
-        (head_rows, 0, HEAD),
-    )
-    bank_order = [first // BANK + b for (rows, first, width) in pieces for b in range(width // BANK)]
+    H0, H1, LEFT, RIGHT = range(BANKS)
+
+    def cols(b):
+        return slice(b * BANK, (b + 1) * BANK)
 
     with ExitStack() as ctx:
         keep = ctx.enter_context(tc.tile_pool(name="keep", bufs=1))
         stage = ctx.enter_context(tc.tile_pool(name="stage", bufs=2))
-        flow = ctx.enter_context(tc.tile_pool(name="flow", bufs=3))
-        psum_gain = ctx.enter_context(tc.psum_pool(name="psum_gain", bufs=1))
-        psum_turn = ctx.enter_context(tc.psum_pool(name="psum_turn", bufs=2))
-        psum_acc = ctx.enter_context(tc.psum_pool(name="psum_acc", bufs=5))
-
-        warm = keep.tile([P, 1], F32)
-        nc.vector.memset(warm[:], 1.0)
-        nc.scalar.activation(out=warm[:], in_=warm[:], func=ACT.Sqrt)
-
-        ident_f32 = keep.tile([P, P], F32)
-        masks.make_identity(nc, ident_f32[:])
-        ones = keep.tile([P, P], BF16)
-        nc.vector.memset(ones[:], 1.0)
-
-        g_row = keep.tile([P, D], BF16)
-        nc.vector.memset(g_row[:], 0.0)
-        nc.scalar.dma_start(out=g_row[0:1, :], in_=g.unsqueeze(0))
-        b_row = keep.tile([P, E], BF16)
-        nc.vector.memset(b_row[:], 0.0)
-        nc.scalar.dma_start(out=b_row[0:1, :], in_=b1.unsqueeze(0))
+        flip = ctx.enter_context(tc.tile_pool(name="flip", bufs=4))
+        psum_turn = ctx.enter_context(tc.psum_pool(name="psum_turn", bufs=4))
+        psum_acc = ctx.enter_context(tc.psum_pool(name="psum_acc", bufs=4))
+        ctx.enter_context(tc.manual_schedule())
 
         x_sb = keep.tile([P, TOK_TILES, D], BF16)
-        for j in range(PAIRS):
-            nc.sync.dma_start(out=x_sb[:, 2 * j : 2 * j + 2, :], in_=x_rows[:, 2 * j : 2 * j + 2, :])
         w_raw = keep.tile([P, PACK, E], BF16)
-        for b in bank_order:
-            cols = slice(b * BANK, (b + 1) * BANK)
-            nc.sync.dma_start(out=w_raw[:, :, cols], in_=w_rows[:, :, cols])
 
-        gain = psum_gain.tile([P, D], F32)
-        nc.tensor.matmul(out=gain[:], lhsT=ones[:], rhs=g_row[:], start=True, stop=True)
+        def load_x(j):
+            nc.sync.dma_start(out=x_sb[:, 2 * j : 2 * j + 2, :], in_=x_rows[:, 2 * j : 2 * j + 2, :])
+
+        def load_w(b):
+            nc.sync.dma_start(out=w_raw[:, :, cols(b)], in_=w_rows[:, :, cols(b)])
+
+        consts = keep.tile([P, BANK], BF16)
+        nc.vector.memset(consts[:], 0.0)
+        warm = keep.tile([P, 1], F32)
+        nc.vector.memset(warm[:], 1.0)
+        nc.scalar.activation(out=warm[:], in_=warm[:], func=ACT.Abs_reciprocal_sqrt)
+
+        load_x(0)
+        nc.sync.dma_start(out=consts[GAIN_ROW : GAIN_ROW + 1, :], in_=g.unsqueeze(0))
+        nc.sync.dma_start(out=consts[0:BANKS, :], in_=b1.rearrange("(r c) -> r c", c=BANK))
+        load_w(LEFT)
+        load_x(1)
+        load_w(RIGHT)
+        load_x(2)
+        load_x(3)
+        load_w(H0)
+        load_w(H1)
+
+        ident = keep.tile([P, P], BF16)
+        masks.make_identity(nc, ident[:])
+        ident_f32 = keep.tile([P, P], F32)
+        masks.make_identity(nc, ident_f32[:])
+        minus_half = keep.tile([P, 2], F32)
+        nc.gpsimd.memset(minus_half[:], -0.5)
+
+        gain = keep.tile([P, D], BF16)
         bias = keep.tile([P, E], F32)
-        for b in bank_order:
-            cols = slice(b * BANK, (b + 1) * BANK)
-            acc = psum_acc.tile([P, BANK], F32, tag="acc")
-            nc.tensor.matmul(out=acc[:], lhsT=ones[:], rhs=b_row[:, cols], start=True, stop=True)
-            nc.vector.tensor_copy(out=bias[:, cols], in_=acc[:])
+        bias_col = keep.tile([P, GROUPS, 2], F32)
+
+        def spread(row, out, copy):
+            acc = psum_acc.tile([P, BANK], F32, tag="acc", name="acc")
+            nc.tensor.matmul(
+                out=acc[:], lhsT=ident[:, row : row + 1].to_broadcast([P, P]), rhs=consts[:], start=True, stop=True
+            )
+            copy(out=out, in_=acc[:])
+
+        def bias_columns():
+            turned = psum_turn.tile([P, GROUPS, P], BF16, tag="turn", name="turn")
+            for c in range(GROUPS):
+                nc.tensor.transpose(turned[:, c, :], consts[:, c * P : (c + 1) * P], ident[:])
+            nc.vector.tensor_copy(out=bias_col[:], in_=turned[:, :, 0:2])
 
         x_codes = keep.tile([P, TOKENS], U32, align_bytes=64)
         x_scales = keep.tile([P, TOKENS], U8, align_bytes=64)
@@ -92,18 +112,36 @@ def tile_avey_pa_kernel(tc, x, g, W1, b1, out_0, out_1, out_2):
 
         squares = keep.tile([P, TOK_TILES, D], BF16)
         sumsq = keep.tile([P, TOK_TILES], F32)
-        rms = keep.tile([P, TOK_TILES], F32)
         rstd = keep.tile([P, TOK_TILES], F32)
+        x_grouped = [keep.tile([P, 2, P, PACK], BF16, align_bytes=64, name="x_grouped%d" % j) for j in range(PAIRS)]
+        w_grouped = [keep.tile([P, BANK, PACK], BF16, align_bytes=64, name="w_grouped%d" % b) for b in range(BANKS)]
 
-        def normalise_pair(j):
+        def x_stats(j):
             pair = slice(2 * j, 2 * j + 2)
-            for i in (2 * j, 2 * j + 1):
-                nc.scalar.activation(
-                    out=squares[:, i, :], in_=x_sb[:, i, :], func=ACT.Square, accum_out=sumsq[:, i : i + 1]
+            nc.scalar.activation(
+                out=squares[:, 2 * j, :], in_=x_sb[:, 2 * j, :], func=ACT.Square, accum_out=sumsq[:, 2 * j : 2 * j + 1]
+            )
+            odd = slice(2 * j + 1, 2 * j + 2)
+            if j == 0:
+                nc.vector.scalar_tensor_tensor(
+                    out=squares[:, 1, :],
+                    in0=x_sb[:, 1, :],
+                    scalar=1.0,
+                    in1=x_sb[:, 1, :],
+                    op0=ALU.mult,
+                    op1=ALU.mult,
+                    accum_out=sumsq[:, odd],
                 )
-            nc.scalar.activation(out=rms[:, pair], in_=sumsq[:, pair], func=ACT.Sqrt, bias=EPS_RMS, scale=1.0 / D)
-            nc.vector.reciprocal(out=rstd[:, pair], in_=rms[:, pair])
-            xn = stage.tile([P, 2, D], BF16)
+            else:
+                nc.scalar.activation(
+                    out=squares[:, 2 * j + 1, :], in_=x_sb[:, 2 * j + 1, :], func=ACT.Square, accum_out=sumsq[:, odd]
+                )
+            nc.scalar.activation(
+                out=rstd[:, pair], in_=sumsq[:, pair], func=ACT.Abs_reciprocal_sqrt, bias=EPS_RMS, scale=1.0 / D
+            )
+
+        def x_turn(j):
+            xn = stage.tile([P, 2, D], BF16, name="xn")
             for h in range(2):
                 i = 2 * j + h
                 nc.vector.scalar_tensor_tensor(
@@ -115,87 +153,218 @@ def tile_avey_pa_kernel(tc, x, g, W1, b1, out_0, out_1, out_2):
                     op1=ALU.mult,
                 )
             words = xn[:].bitcast(F32)
-            turned = psum_turn.tile([P, 2, 2, P], F32)
+            turned = psum_turn.tile([P, 2, 2, P], F32, tag="turn", name="turn")
             for h in range(2):
                 for u in range(2):
                     nc.tensor.transpose(turned[:, h, u, :], words[:, h, u::2], ident_f32[:])
-            x_grouped = stage.tile([P, 2, P, PACK], BF16, align_bytes=64)
-            nc.scalar.copy(out=x_grouped[:].bitcast(F32), in_=turned[:].rearrange("p h u r -> p h r u"))
+            nc.scalar.copy(
+                out=x_grouped[j][:].rearrange("p h r t -> p (h r t)").bitcast(F32),
+                in_=turned[:].rearrange("p h u r -> p h r u"),
+            )
+
+        def x_quantise(j):
             toks = slice(2 * j * P, (2 * j + 2) * P)
             nc.vector.quantize_mx(
                 out=x_codes[:, toks].bitcast(FP8X4),
                 scales=x_scales[:, toks],
-                in_=x_grouped[:].rearrange("p h r t -> p (h r t)"),
+                in_=x_grouped[j][:].rearrange("p h r t -> p (h r t)"),
+            )
+            ready.update((("x", 2 * j), ("x", 2 * j + 1)))
+
+        def w_group(b, copy):
+            copy(
+                out=w_grouped[b][:].rearrange("p (c i) t -> p c t i", i=4),
+                in_=w_raw[:, :, cols(b)].rearrange("p t (c i) -> p c t i", i=4),
             )
 
-        def quantise_w_bank(b):
-            cols = slice(b * BANK, (b + 1) * BANK)
-            w_grouped = stage.tile([P, BANK, PACK], BF16, align_bytes=64)
-            nc.vector.tensor_copy(
-                out=w_grouped[:].rearrange("p (c i) t -> p c t i", i=4),
-                in_=w_raw[:, :, cols].rearrange("p t (c i) -> p c t i", i=4),
-            )
+        def w_quantise(b):
             nc.vector.quantize_mx(
-                out=w_codes[:, cols].bitcast(FP8X4),
-                scales=w_scales[:, cols],
-                in_=w_grouped[:].rearrange("p f t -> p (f t)"),
+                out=w_codes[:, cols(b)].bitcast(FP8X4),
+                scales=w_scales[:, cols(b)],
+                in_=w_grouped[b][:].rearrange("p f t -> p (f t)"),
             )
+            ready.add(("w", b))
 
+        pre = keep.tile([P, TOK_TILES, HEAD], F32)
+        enriched = keep.tile([P, TOK_TILES, E], F32)
+        fourth = keep.tile([P, TOK_TILES, HALF], BF16)
+        unit_rows = keep.tile([P, TOK_TILES, HALF], F32)
         norm2 = keep.tile([P, TOK_TILES], F32)
         norm2_floor = keep.tile([P, TOK_TILES], F32)
-        norm = keep.tile([P, TOK_TILES], F32)
         inv_norm = keep.tile([P, TOK_TILES], F32)
+        ready = set()
+        accs = {}
 
-        def enrich_tile(i):
-            toks = slice(i * P, (i + 1) * P)
-            one = slice(i, i + 1)
-            pre = flow.tile([P, E], F32)
-            enriched = flow.tile([P, E], F32)
-            for rows, first, width in pieces:
-                span = slice(first, first + width)
-                for b in range(first // BANK, (first + width) // BANK):
-                    cols = slice(b * BANK, (b + 1) * BANK)
-                    acc = psum_acc.tile([P, BANK], F32, tag="acc")
-                    nc.tensor.matmul_mx(
-                        out=acc[:],
-                        lhsT=x_codes[:, toks].bitcast(FP8X4),
-                        lhsT_scale=x_scales[:, toks],
-                        rhs=w_codes[:, cols].bitcast(FP8X4),
-                        rhs_scale=w_scales[:, cols],
-                        start=True,
-                        stop=True,
-                    )
-                    nc.vector.tensor_tensor(out=pre[:, cols], in0=acc[:], in1=bias[:, cols], op=ALU.add)
-                nc.gpsimd.tensor_scalar(
-                    out=pre[:, span], in0=pre[:, span], scalar1=FLT_MAX, scalar2=0.0, op0=ALU.min, op1=ALU.max
+        def matmul(unit):
+            acc = psum_acc.tile([P, BANK], F32, tag="acc", name="acc")
+            if len(unit) == 2:
+                i, b = unit
+                toks, feats = slice(i * P, (i + 1) * P), cols(b)
+                nc.tensor.matmul_mx(
+                    out=acc[:],
+                    lhsT=x_codes[:, toks].bitcast(FP8X4),
+                    lhsT_scale=x_scales[:, toks],
+                    rhs=w_codes[:, feats].bitcast(FP8X4),
+                    rhs_scale=w_scales[:, feats],
+                    start=True,
+                    stop=True,
                 )
-                nc.scalar.activation(out=enriched[:, span], in_=pre[:, span], func=ACT.Square)
-                if rows is right_rows:
-                    fourth = flow.tile([P, HALF], BF16)
-                    nc.scalar.activation(
-                        out=fourth[:], in_=enriched[:, span], func=ACT.Square, accum_out=norm2[:, one]
-                    )
-                    nc.vector.tensor_scalar_max(out=norm2_floor[:, one], in0=norm2[:, one], scalar1=EPS_NORM * EPS_NORM)
-                    nc.scalar.activation(out=norm[:, one], in_=norm2_floor[:, one], func=ACT.Sqrt)
-                    nc.vector.reciprocal(out=inv_norm[:, one], in_=norm[:, one])
-                    unit = flow.tile([P, HALF], F32)
-                    nc.gpsimd.tensor_scalar(
-                        out=unit[:],
-                        in0=enriched[:, span],
-                        scalar1=inv_norm[:, one],
-                        scalar2=1.0,
-                        op0=ALU.mult,
-                        op1=ALU.mult,
-                    )
-                    nc.sync.dma_start(out=rows[:, i, :], in_=unit[:])
-                else:
-                    nc.sync.dma_start(out=rows[:, i, :], in_=enriched[:, span])
+            else:
+                q, b, c = unit
+                toks = slice(q * BANK, (q + 1) * BANK)
+                feats = slice(b * BANK + c * P, b * BANK + (c + 1) * P)
+                nc.tensor.matmul_mx(
+                    out=acc[:],
+                    lhsT=w_codes[:, feats].bitcast(FP8X4),
+                    lhsT_scale=w_scales[:, feats],
+                    rhs=x_codes[:, toks].bitcast(FP8X4),
+                    rhs_scale=x_scales[:, toks],
+                    start=True,
+                    stop=True,
+                )
+            accs[unit] = acc
 
-        normalise_pair(0)
-        for b in bank_order:
-            quantise_w_bank(b)
-        for j in range(PAIRS):
-            if j + 1 < PAIRS:
-                normalise_pair(j + 1)
-            enrich_tile(2 * j)
-            enrich_tile(2 * j + 1)
+        def operands_ready(unit):
+            tiles = unit[:1] if len(unit) == 2 else range(QUAD * unit[0], QUAD * (unit[0] + 1))
+            return ("w", unit[1]) in ready and all(("x", i) in ready for i in tiles)
+
+        def token_unit(i, b):
+            here = slice((b - LEFT) * BANK, (b - LEFT + 1) * BANK)
+            nc.vector.tensor_tensor(out=pre[:, i, here], in0=accs[i, b][:], in1=bias[:, cols(b)], op=ALU.add)
+            nc.gpsimd.tensor_scalar(
+                out=pre[:, i, here], in0=pre[:, i, here], scalar1=FLT_MAX, scalar2=0.0, op0=ALU.min, op1=ALU.max
+            )
+            nc.scalar.activation(out=enriched[:, i, cols(b)], in_=pre[:, i, here], func=ACT.Square)
+            if b == LEFT:
+                nc.sync.dma_start(out=left_rows[:, i, :], in_=enriched[:, i, cols(LEFT)])
+            else:
+                nc.scalar.activation(
+                    out=fourth[:, i, :], in_=enriched[:, i, cols(b)], func=ACT.Square, accum_out=norm2[:, i : i + 1]
+                )
+
+        def feature_unit(q, b, c):
+            flipped = flip.tile([P, BANK], F32, name="flipped")
+            nc.vector.tensor_scalar(
+                out=flipped[:],
+                in0=accs[q, b, c][:],
+                scalar1=bias_col[:, c, b : b + 1],
+                scalar2=0.0,
+                op0=ALU.add,
+                op1=ALU.max,
+            )
+            turned = psum_turn.tile([P, QUAD, P], F32, tag="turn", name="turn")
+            for h in range(QUAD):
+                nc.tensor.transpose(turned[:, h, :], flipped[:, h * P : (h + 1) * P], ident_f32[:])
+            quad = slice(QUAD * q, QUAD * (q + 1))
+            feats = slice(b * BANK + c * P, b * BANK + (c + 1) * P)
+            nc.scalar.activation(out=enriched[:, quad, feats], in_=turned[:], func=ACT.Square)
+            if c == GROUPS - 1:
+                for first in (QUAD * q, QUAD * q + 2):
+                    two = slice(first, first + 2)
+                    nc.sync.dma_start(out=head_rows[:, two, cols(b)], in_=enriched[:, two, cols(b)])
+
+        def right_scale(j):
+            pair = slice(2 * j, 2 * j + 2)
+            nc.gpsimd.tensor_scalar(
+                out=norm2_floor[:, pair],
+                in0=norm2[:, pair],
+                scalar1=EPS_NORM * EPS_NORM,
+                scalar2=1.0,
+                op0=ALU.max,
+                op1=ALU.mult,
+            )
+            nc.gpsimd.tensor_tensor(
+                out=inv_norm[:, pair], in0=norm2_floor[:, pair], in1=minus_half[:], op=ALU.pow
+            )
+            for i in (2 * j, 2 * j + 1):
+                nc.gpsimd.tensor_scalar(
+                    out=unit_rows[:, i, :],
+                    in0=enriched[:, i, cols(RIGHT)],
+                    scalar1=inv_norm[:, i : i + 1],
+                    scalar2=1.0,
+                    op0=ALU.mult,
+                    op1=ALU.mult,
+                )
+                nc.sync.dma_start(out=right_rows[:, i, :], in_=unit_rows[:, i, :])
+
+        def features(q, b):
+            return [(q, b, c) for c in range(GROUPS)]
+
+        x_stats(0)
+        spread(GAIN_ROW, gain[:], nc.vector.tensor_copy)
+        spread(LEFT, bias[:, cols(LEFT)], nc.scalar.copy)
+        spread(RIGHT, bias[:, cols(RIGHT)], nc.scalar.copy)
+        x_stats(1)
+        bias_columns()
+        x_turn(0)
+        w_group(LEFT, nc.vector.tensor_copy)
+        x_stats(2)
+        x_quantise(0)
+        w_quantise(LEFT)
+        steps = [
+            (x_turn, 1),
+            (0, LEFT),
+            (1, LEFT),
+            (w_group, RIGHT, nc.vector.tensor_copy),
+            (x_stats, 3),
+            (x_quantise, 1),
+            (2, LEFT),
+            (w_quantise, RIGHT),
+            (3, LEFT),
+            (w_group, H0, nc.vector.tensor_copy),
+            (0, RIGHT),
+            (1, RIGHT),
+            (w_quantise, H0),
+            (x_turn, 2),
+            (2, RIGHT),
+            (3, RIGHT),
+            (right_scale, 0),
+            (0, H0, 0),
+            (0, H0, 1),
+            (x_quantise, 2),
+            (0, H0, 2),
+            (right_scale, 1),
+            (0, H0, 3),
+            (w_group, H1, nc.vector.tensor_copy),
+            (4, RIGHT),
+            (5, RIGHT),
+            (w_quantise, H1),
+            (x_turn, 3),
+            (4, LEFT),
+            (5, LEFT),
+            (right_scale, 2),
+            (0, H1, 0),
+            (0, H1, 1),
+            (x_quantise, 3),
+            (0, H1, 2),
+            (0, H1, 3),
+            (6, RIGHT),
+            (7, RIGHT),
+            (1, H0, 0),
+            (1, H0, 1),
+            (right_scale, 3),
+            (1, H0, 2),
+            (1, H0, 3),
+            (6, LEFT),
+            (1, H1, 0),
+            (1, H1, 1),
+            (1, H1, 2),
+            (1, H1, 3),
+            (7, LEFT),
+        ]
+        is_unit = [isinstance(step[0], int) for step in steps]
+        units = [step for step, u in zip(steps, is_unit) if u]
+        issued = 0
+        worked = 0
+        for step, u in zip(steps, is_unit):
+            while issued < min(worked + LEAD + 1, len(units)) and operands_ready(units[issued]):
+                matmul(units[issued])
+                issued += 1
+            if not u:
+                step[0](*step[1:])
+                continue
+            if len(step) == 2:
+                token_unit(*step)
+            else:
+                feature_unit(*step)
+            worked += 1

@@ -22,13 +22,12 @@ BANK = 512
 TOK_TILES = TOKENS // P
 PAIRS = TOK_TILES // 2
 QUAD = 4
+QUADS = TOK_TILES // QUAD
 GROUPS = BANK // P
-LEAD = 3
 BANKS = E // BANK
 GAIN_ROW = BANKS
 EPS_RMS = 1e-6
 EPS_NORM = 1e-12
-FLT_MAX = 3.4028234663852886e38
 
 FLOPS = 2 * TOKENS * D * E
 
@@ -43,6 +42,7 @@ def tile_avey_pa_kernel(tc, x, g, W1, b1, out_0, out_1, out_2):
     w_rows = W1.rearrange("(p t) f -> p t f", t=PACK)
 
     H0, H1, LEFT, RIGHT = range(BANKS)
+    outputs = {H0: (head_rows, 0), H1: (head_rows, BANK), LEFT: (left_rows, 0)}
 
     def cols(b):
         return slice(b * BANK, (b + 1) * BANK)
@@ -55,14 +55,14 @@ def tile_avey_pa_kernel(tc, x, g, W1, b1, out_0, out_1, out_2):
         psum_acc = ctx.enter_context(tc.psum_pool(name="psum_acc", bufs=4))
         ctx.enter_context(tc.manual_schedule())
 
-        x_sb = keep.tile([P, TOK_TILES, D], BF16)
-        w_raw = keep.tile([P, PACK, E], BF16)
+        x_sb = [keep.tile([P, 2, D], BF16, name="x_sb%d" % j) for j in range(PAIRS)]
+        w_raw = [keep.tile([P, PACK, BANK], BF16, name="w_raw%d" % b) for b in range(BANKS)]
 
         def load_x(j):
-            nc.sync.dma_start(out=x_sb[:, 2 * j : 2 * j + 2, :], in_=x_rows[:, 2 * j : 2 * j + 2, :])
+            nc.sync.dma_start(out=x_sb[j][:], in_=x_rows[:, 2 * j : 2 * j + 2, :])
 
         def load_w(b):
-            nc.sync.dma_start(out=w_raw[:, :, cols(b)], in_=w_rows[:, :, cols(b)])
+            nc.sync.dma_start(out=w_raw[b][:], in_=w_rows[:, :, cols(b)])
 
         consts = keep.tile([P, BANK], BF16)
         nc.vector.memset(consts[:], 0.0)
@@ -75,79 +75,76 @@ def tile_avey_pa_kernel(tc, x, g, W1, b1, out_0, out_1, out_2):
         nc.sync.dma_start(out=consts[0:BANKS, :], in_=b1.rearrange("(r c) -> r c", c=BANK))
         load_w(LEFT)
         load_x(1)
-        load_w(RIGHT)
+        load_w(H0)
         load_x(2)
         load_x(3)
-        load_w(H0)
+        load_w(RIGHT)
         load_w(H1)
 
         ident = keep.tile([P, P], BF16)
         masks.make_identity(nc, ident[:])
         ident_f32 = keep.tile([P, P], F32)
         masks.make_identity(nc, ident_f32[:])
-        minus_half = keep.tile([P, 2], F32)
-        nc.gpsimd.memset(minus_half[:], -0.5)
 
         gain = keep.tile([P, D], BF16)
-        bias = keep.tile([P, E], F32)
-        bias_col = keep.tile([P, GROUPS, 2], F32)
+        bias = keep.tile([P, GROUPS, BANKS], F32)
 
-        def spread(row, out, copy):
+        def spread_gain():
             acc = psum_acc.tile([P, BANK], F32, tag="acc", name="acc")
             nc.tensor.matmul(
-                out=acc[:], lhsT=ident[:, row : row + 1].to_broadcast([P, P]), rhs=consts[:], start=True, stop=True
+                out=acc[:],
+                lhsT=ident[:, GAIN_ROW : GAIN_ROW + 1].to_broadcast([P, P]),
+                rhs=consts[:],
+                start=True,
+                stop=True,
             )
-            copy(out=out, in_=acc[:])
+            nc.vector.tensor_copy(out=gain[:], in_=acc[:])
 
-        def bias_columns():
+        def turn_bias():
             turned = psum_turn.tile([P, GROUPS, P], BF16, tag="turn", name="turn")
             for c in range(GROUPS):
                 nc.tensor.transpose(turned[:, c, :], consts[:, c * P : (c + 1) * P], ident[:])
-            nc.vector.tensor_copy(out=bias_col[:], in_=turned[:, :, 0:2])
+            nc.vector.tensor_copy(out=bias[:], in_=turned[:, :, 0:BANKS])
 
-        x_codes = keep.tile([P, TOKENS], U32, align_bytes=64)
-        x_scales = keep.tile([P, TOKENS], U8, align_bytes=64)
-        w_codes = keep.tile([P, E], U32, align_bytes=64)
-        w_scales = keep.tile([P, E], U8, align_bytes=64)
-
-        squares = keep.tile([P, TOK_TILES, D], BF16)
-        sumsq = keep.tile([P, TOK_TILES], F32)
-        rstd = keep.tile([P, TOK_TILES], F32)
+        x_codes = [keep.tile([P, BANK], U32, align_bytes=64, name="x_codes%d" % q) for q in range(QUADS)]
+        x_scales = [keep.tile([P, BANK], U8, align_bytes=64, name="x_scales%d" % q) for q in range(QUADS)]
+        w_codes = [keep.tile([P, BANK], U32, align_bytes=64, name="w_codes%d" % b) for b in range(BANKS)]
+        w_scales = [keep.tile([P, BANK], U8, align_bytes=64, name="w_scales%d" % b) for b in range(BANKS)]
         x_grouped = [keep.tile([P, 2, P, PACK], BF16, align_bytes=64, name="x_grouped%d" % j) for j in range(PAIRS)]
         w_grouped = [keep.tile([P, BANK, PACK], BF16, align_bytes=64, name="w_grouped%d" % b) for b in range(BANKS)]
+        rstd = [keep.tile([P, 2], F32, name="rstd%d" % j) for j in range(PAIRS)]
 
-        def x_stats(j):
-            pair = slice(2 * j, 2 * j + 2)
+        def x_stats(j, vector_half=False):
+            squares = stage.tile([P, 2, D], BF16, name="squares")
+            sumsq = stage.tile([P, 2], F32, name="sumsq")
             nc.scalar.activation(
-                out=squares[:, 2 * j, :], in_=x_sb[:, 2 * j, :], func=ACT.Square, accum_out=sumsq[:, 2 * j : 2 * j + 1]
+                out=squares[:, 0, :], in_=x_sb[j][:, 0, :], func=ACT.Square, accum_out=sumsq[:, 0:1]
             )
-            odd = slice(2 * j + 1, 2 * j + 2)
-            if j == 0:
+            if vector_half:
                 nc.vector.scalar_tensor_tensor(
                     out=squares[:, 1, :],
-                    in0=x_sb[:, 1, :],
+                    in0=x_sb[j][:, 1, :],
                     scalar=1.0,
-                    in1=x_sb[:, 1, :],
+                    in1=x_sb[j][:, 1, :],
                     op0=ALU.mult,
                     op1=ALU.mult,
-                    accum_out=sumsq[:, odd],
+                    accum_out=sumsq[:, 1:2],
                 )
             else:
                 nc.scalar.activation(
-                    out=squares[:, 2 * j + 1, :], in_=x_sb[:, 2 * j + 1, :], func=ACT.Square, accum_out=sumsq[:, odd]
+                    out=squares[:, 1, :], in_=x_sb[j][:, 1, :], func=ACT.Square, accum_out=sumsq[:, 1:2]
                 )
             nc.scalar.activation(
-                out=rstd[:, pair], in_=sumsq[:, pair], func=ACT.Abs_reciprocal_sqrt, bias=EPS_RMS, scale=1.0 / D
+                out=rstd[j][:], in_=sumsq[:], func=ACT.Abs_reciprocal_sqrt, bias=EPS_RMS, scale=1.0 / D
             )
 
         def x_turn(j):
             xn = stage.tile([P, 2, D], BF16, name="xn")
             for h in range(2):
-                i = 2 * j + h
                 nc.vector.scalar_tensor_tensor(
                     out=xn[:, h, :],
-                    in0=x_sb[:, i, :],
-                    scalar=rstd[:, i : i + 1],
+                    in0=x_sb[j][:, h, :],
+                    scalar=rstd[j][:, h : h + 1],
                     in1=gain[:],
                     op0=ALU.mult,
                     op1=ALU.mult,
@@ -163,208 +160,142 @@ def tile_avey_pa_kernel(tc, x, g, W1, b1, out_0, out_1, out_2):
             )
 
         def x_quantise(j):
-            toks = slice(2 * j * P, (2 * j + 2) * P)
+            here = slice((j % 2) * 2 * P, (j % 2 + 1) * 2 * P)
             nc.vector.quantize_mx(
-                out=x_codes[:, toks].bitcast(FP8X4),
-                scales=x_scales[:, toks],
+                out=x_codes[j // 2][:, here].bitcast(FP8X4),
+                scales=x_scales[j // 2][:, here],
                 in_=x_grouped[j][:].rearrange("p h r t -> p (h r t)"),
             )
-            ready.update((("x", 2 * j), ("x", 2 * j + 1)))
 
-        def w_group(b, copy):
+        def w_group(b, copy, first=0, last=BANK):
             copy(
-                out=w_grouped[b][:].rearrange("p (c i) t -> p c t i", i=4),
-                in_=w_raw[:, :, cols(b)].rearrange("p t (c i) -> p c t i", i=4),
+                out=w_grouped[b][:, first:last, :].rearrange("p (c i) t -> p c t i", i=4),
+                in_=w_raw[b][:, :, first:last].rearrange("p t (c i) -> p c t i", i=4),
             )
 
         def w_quantise(b):
             nc.vector.quantize_mx(
-                out=w_codes[:, cols(b)].bitcast(FP8X4),
-                scales=w_scales[:, cols(b)],
+                out=w_codes[b][:].bitcast(FP8X4),
+                scales=w_scales[b][:],
                 in_=w_grouped[b][:].rearrange("p f t -> p (f t)"),
             )
-            ready.add(("w", b))
 
-        pre = keep.tile([P, TOK_TILES, HEAD], F32)
-        enriched = keep.tile([P, TOK_TILES, E], F32)
-        fourth = keep.tile([P, TOK_TILES, HALF], BF16)
-        unit_rows = keep.tile([P, TOK_TILES, HALF], F32)
-        norm2 = keep.tile([P, TOK_TILES], F32)
-        norm2_floor = keep.tile([P, TOK_TILES], F32)
-        inv_norm = keep.tile([P, TOK_TILES], F32)
-        ready = set()
+        enriched = {}
         accs = {}
 
         def matmul(unit):
+            q, b, c = unit
             acc = psum_acc.tile([P, BANK], F32, tag="acc", name="acc")
-            if len(unit) == 2:
-                i, b = unit
-                toks, feats = slice(i * P, (i + 1) * P), cols(b)
-                nc.tensor.matmul_mx(
-                    out=acc[:],
-                    lhsT=x_codes[:, toks].bitcast(FP8X4),
-                    lhsT_scale=x_scales[:, toks],
-                    rhs=w_codes[:, feats].bitcast(FP8X4),
-                    rhs_scale=w_scales[:, feats],
-                    start=True,
-                    stop=True,
-                )
-            else:
-                q, b, c = unit
-                toks = slice(q * BANK, (q + 1) * BANK)
-                feats = slice(b * BANK + c * P, b * BANK + (c + 1) * P)
-                nc.tensor.matmul_mx(
-                    out=acc[:],
-                    lhsT=w_codes[:, feats].bitcast(FP8X4),
-                    lhsT_scale=w_scales[:, feats],
-                    rhs=x_codes[:, toks].bitcast(FP8X4),
-                    rhs_scale=x_scales[:, toks],
-                    start=True,
-                    stop=True,
-                )
+            feats = slice(c * P, (c + 1) * P)
+            nc.tensor.matmul_mx(
+                out=acc[:],
+                lhsT=w_codes[b][:, feats].bitcast(FP8X4),
+                lhsT_scale=w_scales[b][:, feats],
+                rhs=x_codes[q][:].bitcast(FP8X4),
+                rhs_scale=x_scales[q][:],
+                start=True,
+                stop=True,
+            )
             accs[unit] = acc
 
-        def operands_ready(unit):
-            tiles = unit[:1] if len(unit) == 2 else range(QUAD * unit[0], QUAD * (unit[0] + 1))
-            return ("w", unit[1]) in ready and all(("x", i) in ready for i in tiles)
-
-        def token_unit(i, b):
-            here = slice((b - LEFT) * BANK, (b - LEFT + 1) * BANK)
-            nc.vector.tensor_tensor(out=pre[:, i, here], in0=accs[i, b][:], in1=bias[:, cols(b)], op=ALU.add)
-            nc.gpsimd.tensor_scalar(
-                out=pre[:, i, here], in0=pre[:, i, here], scalar1=FLT_MAX, scalar2=0.0, op0=ALU.min, op1=ALU.max
-            )
-            nc.scalar.activation(out=enriched[:, i, cols(b)], in_=pre[:, i, here], func=ACT.Square)
-            if b == LEFT:
-                nc.sync.dma_start(out=left_rows[:, i, :], in_=enriched[:, i, cols(LEFT)])
-            else:
+        def work(units):
+            flipped = []
+            for q, b, c in units:
+                flat = flip.tile([P, BANK], F32, name="flat")
+                nc.vector.tensor_scalar(
+                    out=flat[:],
+                    in0=accs[q, b, c][:],
+                    scalar1=bias[:, c, b : b + 1],
+                    scalar2=0.0,
+                    op0=ALU.add,
+                    op1=ALU.max,
+                )
+                flipped.append(flat)
+            turns = []
+            for flat in flipped:
+                turned = psum_turn.tile([P, QUAD, P], F32, tag="turn", name="turn")
+                for h in range(QUAD):
+                    nc.tensor.transpose(turned[:, h, :], flat[:, h * P : (h + 1) * P], ident_f32[:])
+                turns.append(turned)
+            for (q, b, c), turned in zip(units, turns):
+                if c == 0:
+                    enriched[q, b] = keep.tile([P, QUAD, BANK], F32, name="enriched%d%d" % (q, b))
                 nc.scalar.activation(
-                    out=fourth[:, i, :], in_=enriched[:, i, cols(b)], func=ACT.Square, accum_out=norm2[:, i : i + 1]
+                    out=enriched[q, b][:, :, c * P : (c + 1) * P], in_=turned[:], func=ACT.Square
                 )
 
-        def feature_unit(q, b, c):
-            flipped = flip.tile([P, BANK], F32, name="flipped")
-            nc.vector.tensor_scalar(
-                out=flipped[:],
-                in0=accs[q, b, c][:],
-                scalar1=bias_col[:, c, b : b + 1],
-                scalar2=0.0,
-                op0=ALU.add,
-                op1=ALU.max,
-            )
-            turned = psum_turn.tile([P, QUAD, P], F32, tag="turn", name="turn")
-            for h in range(QUAD):
-                nc.tensor.transpose(turned[:, h, :], flipped[:, h * P : (h + 1) * P], ident_f32[:])
-            quad = slice(QUAD * q, QUAD * (q + 1))
-            feats = slice(b * BANK + c * P, b * BANK + (c + 1) * P)
-            nc.scalar.activation(out=enriched[:, quad, feats], in_=turned[:], func=ACT.Square)
-            if c == GROUPS - 1:
-                for first in (QUAD * q, QUAD * q + 2):
-                    two = slice(first, first + 2)
-                    nc.sync.dma_start(out=head_rows[:, two, cols(b)], in_=enriched[:, two, cols(b)])
+        def store(q, b, tiles=2):
+            rows, first = outputs[b]
+            for t in range(0, QUAD, tiles):
+                here = slice(t, t + tiles)
+                there = slice(QUAD * q + t, QUAD * q + t + tiles)
+                nc.sync.dma_start(
+                    out=rows[:, there, first : first + BANK], in_=enriched[q, b][:, here, :]
+                )
 
-        def right_scale(j):
-            pair = slice(2 * j, 2 * j + 2)
-            nc.gpsimd.tensor_scalar(
-                out=norm2_floor[:, pair],
-                in0=norm2[:, pair],
-                scalar1=EPS_NORM * EPS_NORM,
-                scalar2=1.0,
-                op0=ALU.max,
-                op1=ALU.mult,
+        norm2 = [keep.tile([P, QUAD], F32, name="norm2_%d" % q) for q in range(QUADS)]
+
+        def right_sums(q, h):
+            fourth = stage.tile([P, HALF], BF16, name="fourth")
+            nc.scalar.activation(
+                out=fourth[:], in_=enriched[q, RIGHT][:, h, :], func=ACT.Square, accum_out=norm2[q][:, h : h + 1]
             )
-            nc.gpsimd.tensor_tensor(
-                out=inv_norm[:, pair], in0=norm2_floor[:, pair], in1=minus_half[:], op=ALU.pow
-            )
-            for i in (2 * j, 2 * j + 1):
+
+        def right_scale(q):
+            floor = EPS_NORM * EPS_NORM
+            above = stage.tile([P, QUAD], F32, name="above")
+            nc.scalar.activation(out=above[:], in_=norm2[q][:], func=ACT.Relu, bias=-floor)
+            inv_norm = stage.tile([P, QUAD], F32, name="inv_norm")
+            nc.scalar.activation(out=inv_norm[:], in_=above[:], func=ACT.Abs_reciprocal_sqrt, bias=floor)
+            for h in range(QUAD):
+                unit_rows = keep.tile([P, HALF], F32, name="unit_rows%d%d" % (q, h))
                 nc.gpsimd.tensor_scalar(
-                    out=unit_rows[:, i, :],
-                    in0=enriched[:, i, cols(RIGHT)],
-                    scalar1=inv_norm[:, i : i + 1],
+                    out=unit_rows[:],
+                    in0=enriched[q, RIGHT][:, h, :],
+                    scalar1=inv_norm[:, h : h + 1],
                     scalar2=1.0,
                     op0=ALU.mult,
                     op1=ALU.mult,
                 )
-                nc.sync.dma_start(out=right_rows[:, i, :], in_=unit_rows[:, i, :])
+                nc.sync.dma_start(out=right_rows[:, QUAD * q + h, :], in_=unit_rows[:])
 
-        def features(q, b):
-            return [(q, b, c) for c in range(GROUPS)]
-
-        x_stats(0)
-        spread(GAIN_ROW, gain[:], nc.vector.tensor_copy)
-        spread(LEFT, bias[:, cols(LEFT)], nc.scalar.copy)
-        spread(RIGHT, bias[:, cols(RIGHT)], nc.scalar.copy)
-        x_stats(1)
-        bias_columns()
+        V = nc.vector.tensor_copy
+        S = nc.scalar.copy
+        x_stats(0, vector_half=True)
+        spread_gain()
+        turn_bias()
         x_turn(0)
-        w_group(LEFT, nc.vector.tensor_copy)
-        x_stats(2)
+        x_stats(1)
+        w_group(LEFT, V)
         x_quantise(0)
+        x_turn(1)
         w_quantise(LEFT)
-        steps = [
-            (x_turn, 1),
-            (0, LEFT),
-            (1, LEFT),
-            (w_group, RIGHT, nc.vector.tensor_copy),
-            (x_stats, 3),
-            (x_quantise, 1),
-            (2, LEFT),
-            (w_quantise, RIGHT),
-            (3, LEFT),
-            (w_group, H0, nc.vector.tensor_copy),
-            (0, RIGHT),
-            (1, RIGHT),
-            (w_quantise, H0),
-            (x_turn, 2),
-            (2, RIGHT),
-            (3, RIGHT),
-            (right_scale, 0),
-            (0, H0, 0),
-            (0, H0, 1),
-            (x_quantise, 2),
-            (0, H0, 2),
-            (right_scale, 1),
-            (0, H0, 3),
-            (w_group, H1, nc.vector.tensor_copy),
-            (4, RIGHT),
-            (5, RIGHT),
-            (w_quantise, H1),
-            (x_turn, 3),
-            (4, LEFT),
-            (5, LEFT),
-            (right_scale, 2),
-            (0, H1, 0),
-            (0, H1, 1),
-            (x_quantise, 3),
-            (0, H1, 2),
-            (0, H1, 3),
-            (6, RIGHT),
-            (7, RIGHT),
-            (1, H0, 0),
-            (1, H0, 1),
-            (right_scale, 3),
-            (1, H0, 2),
-            (1, H0, 3),
-            (6, LEFT),
-            (1, H1, 0),
-            (1, H1, 1),
-            (1, H1, 2),
-            (1, H1, 3),
-            (7, LEFT),
-        ]
-        is_unit = [isinstance(step[0], int) for step in steps]
-        units = [step for step, u in zip(steps, is_unit) if u]
-        issued = 0
-        worked = 0
-        for step, u in zip(steps, is_unit):
-            while issued < min(worked + LEAD + 1, len(units)) and operands_ready(units[issued]):
-                matmul(units[issued])
-                issued += 1
-            if not u:
-                step[0](*step[1:])
-                continue
-            if len(step) == 2:
-                token_unit(*step)
-            else:
-                feature_unit(*step)
-            worked += 1
+        w_group(H0, S, BANK // 2, BANK)
+        w_group(H0, V, 0, BANK // 2)
+        x_quantise(1)
+        x_stats(2)
+        pairs = [((q, b, c), (q, b, c + 1)) for q, b in [(0, LEFT), (0, H0), (0, RIGHT), (1, LEFT), (1, H0), (1, RIGHT), (0, H1), (1, H1)] for c in (0, 2)]
+        beside = {
+            0: [(w_quantise, H0), (x_stats, 3)],
+            1: [(store, 0, LEFT), (x_turn, 2)],
+            2: [(w_group, RIGHT, V), (w_quantise, RIGHT)],
+            3: [(store, 0, H0), (x_quantise, 2), (x_turn, 3)],
+            4: [(x_quantise, 3)],
+            6: [(right_sums, 0, 0), (right_sums, 0, 1)],
+            7: [(right_sums, 0, 2), (right_sums, 0, 3), (store, 1, LEFT), (right_scale, 0)],
+            8: [(w_group, H1, V)],
+            9: [(store, 1, H0), (w_quantise, H1)],
+            12: [(right_sums, 1, 0), (right_sums, 1, 1)],
+            13: [(store, 0, H1), (right_sums, 1, 2), (right_sums, 1, 3), (right_scale, 1)],
+            15: [(store, 1, H1)],
+        }
+        for n, units in enumerate(pairs):
+            if n == 0:
+                for unit in units:
+                    matmul(unit)
+            if n + 1 < len(pairs):
+                for unit in pairs[n + 1]:
+                    matmul(unit)
+            work(units)
+            for step, *args in beside.get(n, ()):
+                step(*args)

@@ -21,9 +21,8 @@ E = HEAD + HALF + HALF
 BANK = 512
 TOK_TILES = TOKENS // P
 PAIRS = TOK_TILES // 2
-QUAD = 4
-QUADS = TOK_TILES // QUAD
 GROUPS = BANK // P
+LEAD = 1
 BANKS = E // BANK
 GAIN_ROW = BANKS
 EPS_RMS = 1e-6
@@ -75,10 +74,10 @@ def tile_avey_pa_kernel(tc, x, g, W1, b1, out_0, out_1, out_2):
         nc.sync.dma_start(out=consts[0:BANKS, :], in_=b1.rearrange("(r c) -> r c", c=BANK))
         load_w(LEFT)
         load_x(1)
-        load_w(H0)
-        load_x(2)
-        load_x(3)
         load_w(RIGHT)
+        load_x(2)
+        load_w(H0)
+        load_x(3)
         load_w(H1)
 
         ident = keep.tile([P, P], BF16)
@@ -106,8 +105,10 @@ def tile_avey_pa_kernel(tc, x, g, W1, b1, out_0, out_1, out_2):
                 nc.tensor.transpose(turned[:, c, :], consts[:, c * P : (c + 1) * P], ident[:])
             nc.vector.tensor_copy(out=bias[:], in_=turned[:, :, 0:BANKS])
 
-        x_codes = [keep.tile([P, BANK], U32, align_bytes=64, name="x_codes%d" % q) for q in range(QUADS)]
-        x_scales = [keep.tile([P, BANK], U8, align_bytes=64, name="x_scales%d" % q) for q in range(QUADS)]
+        ready = set()
+
+        x_codes = [keep.tile([P, 2 * P], U32, align_bytes=64, name="x_codes%d" % j) for j in range(PAIRS)]
+        x_scales = [keep.tile([P, 2 * P], U8, align_bytes=64, name="x_scales%d" % j) for j in range(PAIRS)]
         w_codes = [keep.tile([P, BANK], U32, align_bytes=64, name="w_codes%d" % b) for b in range(BANKS)]
         w_scales = [keep.tile([P, BANK], U8, align_bytes=64, name="w_scales%d" % b) for b in range(BANKS)]
         x_grouped = [keep.tile([P, 2, P, PACK], BF16, align_bytes=64, name="x_grouped%d" % j) for j in range(PAIRS)]
@@ -160,12 +161,12 @@ def tile_avey_pa_kernel(tc, x, g, W1, b1, out_0, out_1, out_2):
             )
 
         def x_quantise(j):
-            here = slice((j % 2) * 2 * P, (j % 2 + 1) * 2 * P)
             nc.vector.quantize_mx(
-                out=x_codes[j // 2][:, here].bitcast(FP8X4),
-                scales=x_scales[j // 2][:, here],
+                out=x_codes[j][:].bitcast(FP8X4),
+                scales=x_scales[j][:],
                 in_=x_grouped[j][:].rearrange("p h r t -> p (h r t)"),
             )
+            ready.add(("x", j))
 
         def w_group(b, copy, first=0, last=BANK):
             copy(
@@ -179,123 +180,155 @@ def tile_avey_pa_kernel(tc, x, g, W1, b1, out_0, out_1, out_2):
                 scales=w_scales[b][:],
                 in_=w_grouped[b][:].rearrange("p f t -> p (f t)"),
             )
+            ready.add(("w", b))
 
         enriched = {}
         accs = {}
 
-        def matmul(unit):
-            q, b, c = unit
-            acc = psum_acc.tile([P, BANK], F32, tag="acc", name="acc")
-            feats = slice(c * P, (c + 1) * P)
-            nc.tensor.matmul_mx(
-                out=acc[:],
-                lhsT=w_codes[b][:, feats].bitcast(FP8X4),
-                lhsT_scale=w_scales[b][:, feats],
-                rhs=x_codes[q][:].bitcast(FP8X4),
-                rhs_scale=x_scales[q][:],
-                start=True,
-                stop=True,
-            )
-            accs[unit] = acc
+        def matmul(j, b):
+            accs[j, b] = []
+            for c in range(0, GROUPS, 2):
+                acc = psum_acc.tile([P, 2, 2 * P], F32, tag="acc", name="acc")
+                for h in range(2):
+                    feats = slice((c + h) * P, (c + h + 1) * P)
+                    nc.tensor.matmul_mx(
+                        out=acc[:, h, :],
+                        lhsT=w_codes[b][:, feats].bitcast(FP8X4),
+                        lhsT_scale=w_scales[b][:, feats],
+                        rhs=x_codes[j][:].bitcast(FP8X4),
+                        rhs_scale=x_scales[j][:],
+                        start=True,
+                        stop=True,
+                    )
+                accs[j, b].append(acc)
 
-        def work(units):
-            flipped = []
-            for q, b, c in units:
-                flat = flip.tile([P, BANK], F32, name="flat")
-                nc.vector.tensor_scalar(
-                    out=flat[:],
-                    in0=accs[q, b, c][:],
-                    scalar1=bias[:, c, b : b + 1],
-                    scalar2=0.0,
-                    op0=ALU.add,
-                    op1=ALU.max,
-                )
-                flipped.append(flat)
-            turns = []
-            for flat in flipped:
-                turned = psum_turn.tile([P, QUAD, P], F32, tag="turn", name="turn")
-                for h in range(QUAD):
-                    nc.tensor.transpose(turned[:, h, :], flat[:, h * P : (h + 1) * P], ident_f32[:])
-                turns.append(turned)
-            for (q, b, c), turned in zip(units, turns):
-                if c == 0:
-                    enriched[q, b] = keep.tile([P, QUAD, BANK], F32, name="enriched%d%d" % (q, b))
+        def work(j, b):
+            flats = []
+            for n, acc in enumerate(accs[j, b]):
+                flat = flip.tile([P, 2, 2 * P], F32, name="flat")
+                for h in range(2):
+                    nc.vector.tensor_scalar(
+                        out=flat[:, h, :],
+                        in0=acc[:, h, :],
+                        scalar1=bias[:, 2 * n + h, b : b + 1],
+                        scalar2=0.0,
+                        op0=ALU.add,
+                        op1=ALU.max,
+                    )
+                flats.append(flat)
+            enriched[j, b] = keep.tile([P, 2, BANK], F32, name="enriched%d%d" % (j, b))
+            for n, flat in enumerate(flats):
+                turned = psum_turn.tile([P, 2, 2, P], F32, tag="turn", name="turn")
+                for h in range(2):
+                    for i in range(2):
+                        nc.tensor.transpose(turned[:, i, h, :], flat[:, h, i * P : (i + 1) * P], ident_f32[:])
                 nc.scalar.activation(
-                    out=enriched[q, b][:, :, c * P : (c + 1) * P], in_=turned[:], func=ACT.Square
+                    out=enriched[j, b][:, :, 2 * n * P : 2 * (n + 1) * P],
+                    in_=turned[:].rearrange("p i h r -> p i (h r)"),
+                    func=ACT.Square,
                 )
 
-        def store(q, b, tiles=2):
+        def store(j, b):
             rows, first = outputs[b]
-            for t in range(0, QUAD, tiles):
-                here = slice(t, t + tiles)
-                there = slice(QUAD * q + t, QUAD * q + t + tiles)
-                nc.sync.dma_start(
-                    out=rows[:, there, first : first + BANK], in_=enriched[q, b][:, here, :]
-                )
-
-        norm2 = [keep.tile([P, QUAD], F32, name="norm2_%d" % q) for q in range(QUADS)]
-
-        def right_sums(q, h):
-            fourth = stage.tile([P, HALF], BF16, name="fourth")
-            nc.scalar.activation(
-                out=fourth[:], in_=enriched[q, RIGHT][:, h, :], func=ACT.Square, accum_out=norm2[q][:, h : h + 1]
+            nc.sync.dma_start(
+                out=rows[:, 2 * j : 2 * j + 2, first : first + BANK], in_=enriched[j, b][:]
             )
 
-        def right_scale(q):
+        norm2 = [keep.tile([P, 2], F32, name="norm2_%d" % j) for j in range(PAIRS)]
+
+        def right_sums(j):
+            fourth = stage.tile([P, 2, HALF], BF16, name="fourth")
+            for i in range(2):
+                nc.scalar.activation(
+                    out=fourth[:, i, :],
+                    in_=enriched[j, RIGHT][:, i, :],
+                    func=ACT.Square,
+                    accum_out=norm2[j][:, i : i + 1],
+                )
+
+        def right_scale(j):
             floor = EPS_NORM * EPS_NORM
-            above = stage.tile([P, QUAD], F32, name="above")
-            nc.scalar.activation(out=above[:], in_=norm2[q][:], func=ACT.Relu, bias=-floor)
-            inv_norm = stage.tile([P, QUAD], F32, name="inv_norm")
+            above = stage.tile([P, 2], F32, name="above")
+            nc.scalar.activation(out=above[:], in_=norm2[j][:], func=ACT.Relu, bias=-floor)
+            inv_norm = stage.tile([P, 2], F32, name="inv_norm")
             nc.scalar.activation(out=inv_norm[:], in_=above[:], func=ACT.Abs_reciprocal_sqrt, bias=floor)
-            for h in range(QUAD):
-                unit_rows = keep.tile([P, HALF], F32, name="unit_rows%d%d" % (q, h))
+            for i in range(2):
+                unit_rows = keep.tile([P, HALF], F32, name="unit_rows%d%d" % (j, i))
                 nc.gpsimd.tensor_scalar(
                     out=unit_rows[:],
-                    in0=enriched[q, RIGHT][:, h, :],
-                    scalar1=inv_norm[:, h : h + 1],
+                    in0=enriched[j, RIGHT][:, i, :],
+                    scalar1=inv_norm[:, i : i + 1],
                     scalar2=1.0,
                     op0=ALU.mult,
                     op1=ALU.mult,
                 )
-                nc.sync.dma_start(out=right_rows[:, QUAD * q + h, :], in_=unit_rows[:])
+                nc.sync.dma_start(out=right_rows[:, 2 * j + i, :], in_=unit_rows[:])
 
         V = nc.vector.tensor_copy
         S = nc.scalar.copy
         x_stats(0, vector_half=True)
         spread_gain()
         turn_bias()
+        w_group(LEFT, S, BANK // 2, BANK)
         x_turn(0)
+        w_group(LEFT, V, 0, BANK // 2)
         x_stats(1)
-        w_group(LEFT, V)
         x_quantise(0)
-        x_turn(1)
         w_quantise(LEFT)
-        w_group(H0, S, BANK // 2, BANK)
-        w_group(H0, V, 0, BANK // 2)
-        x_quantise(1)
-        x_stats(2)
-        pairs = [((q, b, c), (q, b, c + 1)) for q, b in [(0, LEFT), (0, H0), (0, RIGHT), (1, LEFT), (1, H0), (1, RIGHT), (0, H1), (1, H1)] for c in (0, 2)]
-        beside = {
-            0: [(w_quantise, H0), (x_stats, 3)],
-            1: [(store, 0, LEFT), (x_turn, 2)],
-            2: [(w_group, RIGHT, V), (w_quantise, RIGHT)],
-            3: [(store, 0, H0), (x_quantise, 2), (x_turn, 3)],
-            4: [(x_quantise, 3)],
-            6: [(right_sums, 0, 0), (right_sums, 0, 1)],
-            7: [(right_sums, 0, 2), (right_sums, 0, 3), (store, 1, LEFT), (right_scale, 0)],
-            8: [(w_group, H1, V)],
-            9: [(store, 1, H0), (w_quantise, H1)],
-            12: [(right_sums, 1, 0), (right_sums, 1, 1)],
-            13: [(store, 0, H1), (right_sums, 1, 2), (right_sums, 1, 3), (right_scale, 1)],
-            15: [(store, 1, H1)],
-        }
-        for n, units in enumerate(pairs):
-            if n == 0:
-                for unit in units:
-                    matmul(unit)
-            if n + 1 < len(pairs):
-                for unit in pairs[n + 1]:
-                    matmul(unit)
-            work(units)
-            for step, *args in beside.get(n, ()):
-                step(*args)
+        steps = [
+            (x_turn, 1),
+            (0, LEFT),
+            (w_group, RIGHT, S, BANK // 2, BANK),
+            (w_group, RIGHT, V, 0, BANK // 2),
+            (x_quantise, 1),
+            (x_stats, 2),
+            (1, LEFT),
+            (w_quantise, RIGHT),
+            (x_stats, 3),
+            (w_group, H0, V),
+            (0, RIGHT),
+            (x_turn, 2),
+            (1, RIGHT),
+            (w_quantise, H0),
+            (right_sums, 0),
+            (x_quantise, 2),
+            (0, H0),
+            (right_scale, 0),
+            (right_sums, 1),
+            (x_turn, 3),
+            (1, H0),
+            (right_scale, 1),
+            (2, LEFT),
+            (w_group, H1, V),
+            (x_quantise, 3),
+            (2, RIGHT),
+            (w_quantise, H1),
+            (2, H0),
+            (right_sums, 2),
+            (3, RIGHT),
+            (right_scale, 2),
+            (0, H1),
+            (right_sums, 3),
+            (1, H1),
+            (right_scale, 3),
+            (2, H1),
+            (3, H0),
+            (3, H1),
+            (3, LEFT),
+        ]
+        groups = [step for step in steps if isinstance(step[0], int)]
+        issued = worked = 0
+        for step in steps:
+            while issued < min(worked + LEAD + 1, len(groups)) and {
+                ("x", groups[issued][0]),
+                ("w", groups[issued][1]),
+            } <= ready:
+                matmul(*groups[issued])
+                issued += 1
+            if isinstance(step[0], int):
+                work(*step)
+                worked += 1
+                if step[1] != RIGHT:
+                    store(*step)
+            else:
+                step[0](*step[1:])

@@ -20,9 +20,11 @@ HALF = 512
 E = HEAD + HALF + HALF
 BANK = 512
 TOK_TILES = TOKENS // P
+LAST_TOKENS = (4, 5, 6, 7)
+FLT_MAX = 3.4028234663852886e38
 PAIRS = TOK_TILES // 2
+QUAD = 4
 GROUPS = BANK // P
-LEAD = 1
 BANKS = E // BANK
 GAIN_ROW = BANKS
 EPS_RMS = 1e-6
@@ -41,7 +43,8 @@ def tile_avey_pa_kernel(tc, x, g, W1, b1, out_0, out_1, out_2):
     w_rows = W1.rearrange("(p t) f -> p t f", t=PACK)
 
     H0, H1, LEFT, RIGHT = range(BANKS)
-    outputs = {H0: (head_rows, 0), H1: (head_rows, BANK), LEFT: (left_rows, 0)}
+    UNIT = BANKS
+    outputs = {H0: (head_rows, 0), H1: (head_rows, BANK), LEFT: (left_rows, 0), UNIT: (right_rows, 0)}
 
     def cols(b):
         return slice(b * BANK, (b + 1) * BANK)
@@ -50,6 +53,7 @@ def tile_avey_pa_kernel(tc, x, g, W1, b1, out_0, out_1, out_2):
         keep = ctx.enter_context(tc.tile_pool(name="keep", bufs=1))
         stage = ctx.enter_context(tc.tile_pool(name="stage", bufs=2))
         flip = ctx.enter_context(tc.tile_pool(name="flip", bufs=4))
+        tokens = ctx.enter_context(tc.tile_pool(name="tokens", bufs=3))
         psum_turn = ctx.enter_context(tc.psum_pool(name="psum_turn", bufs=4))
         psum_acc = ctx.enter_context(tc.psum_pool(name="psum_acc", bufs=4))
         ctx.enter_context(tc.manual_schedule())
@@ -74,9 +78,9 @@ def tile_avey_pa_kernel(tc, x, g, W1, b1, out_0, out_1, out_2):
         nc.sync.dma_start(out=consts[0:BANKS, :], in_=b1.rearrange("(r c) -> r c", c=BANK))
         load_w(LEFT)
         load_x(1)
-        load_w(RIGHT)
-        load_x(2)
         load_w(H0)
+        load_x(2)
+        load_w(RIGHT)
         load_x(3)
         load_w(H1)
 
@@ -88,27 +92,29 @@ def tile_avey_pa_kernel(tc, x, g, W1, b1, out_0, out_1, out_2):
         gain = keep.tile([P, D], BF16)
         bias = keep.tile([P, GROUPS, BANKS], F32)
 
-        def spread_gain():
-            acc = psum_acc.tile([P, BANK], F32, tag="acc", name="acc")
+        token_bias = keep.tile([P, BANK], BF16)
+
+        def spread(row):
+            acc = psum_acc.tile([P, BANK], BF16, tag="acc", name="acc")
             nc.tensor.matmul(
                 out=acc[:],
-                lhsT=ident[:, GAIN_ROW : GAIN_ROW + 1].to_broadcast([P, P]),
+                lhsT=ident[:, row : row + 1].to_broadcast([P, P]),
                 rhs=consts[:],
                 start=True,
                 stop=True,
             )
-            nc.vector.tensor_copy(out=gain[:], in_=acc[:])
+            return acc
 
         def turn_bias():
             turned = psum_turn.tile([P, GROUPS, P], BF16, tag="turn", name="turn")
             for c in range(GROUPS):
                 nc.tensor.transpose(turned[:, c, :], consts[:, c * P : (c + 1) * P], ident[:])
-            nc.vector.tensor_copy(out=bias[:], in_=turned[:, :, 0:BANKS])
+            return turned
 
         ready = set()
 
-        x_codes = [keep.tile([P, 2 * P], U32, align_bytes=64, name="x_codes%d" % j) for j in range(PAIRS)]
-        x_scales = [keep.tile([P, 2 * P], U8, align_bytes=64, name="x_scales%d" % j) for j in range(PAIRS)]
+        x_codes = [keep.tile([P, BANK], U32, align_bytes=64, name="x_codes%d" % q) for q in range(TOK_TILES // QUAD)]
+        x_scales = [keep.tile([P, BANK], U8, align_bytes=64, name="x_scales%d" % q) for q in range(TOK_TILES // QUAD)]
         w_codes = [keep.tile([P, BANK], U32, align_bytes=64, name="w_codes%d" % b) for b in range(BANKS)]
         w_scales = [keep.tile([P, BANK], U8, align_bytes=64, name="w_scales%d" % b) for b in range(BANKS)]
         x_grouped = [keep.tile([P, 2, P, PACK], BF16, align_bytes=64, name="x_grouped%d" % j) for j in range(PAIRS)]
@@ -139,8 +145,11 @@ def tile_avey_pa_kernel(tc, x, g, W1, b1, out_0, out_1, out_2):
                 out=rstd[j][:], in_=sumsq[:], func=ACT.Abs_reciprocal_sqrt, bias=EPS_RMS, scale=1.0 / D
             )
 
-        def x_turn(j):
-            xn = stage.tile([P, 2, D], BF16, name="xn")
+        xns = {}
+        turneds = {}
+
+        def x_norm(j):
+            xns[j] = xn = stage.tile([P, 2, D], BF16, name="xn")
             for h in range(2):
                 nc.vector.scalar_tensor_tensor(
                     out=xn[:, h, :],
@@ -150,20 +159,30 @@ def tile_avey_pa_kernel(tc, x, g, W1, b1, out_0, out_1, out_2):
                     op0=ALU.mult,
                     op1=ALU.mult,
                 )
-            words = xn[:].bitcast(F32)
+
+        def x_turn(j):
+            words = xns[j][:].bitcast(F32)
             turned = psum_turn.tile([P, 2, 2, P], F32, tag="turn", name="turn")
             for h in range(2):
                 for u in range(2):
                     nc.tensor.transpose(turned[:, h, u, :], words[:, h, u::2], ident_f32[:])
+            turneds[j] = turned
+
+        def x_copy(j):
             nc.scalar.copy(
                 out=x_grouped[j][:].rearrange("p h r t -> p (h r t)").bitcast(F32),
-                in_=turned[:].rearrange("p h u r -> p h r u"),
+                in_=turneds[j][:].rearrange("p h u r -> p h r u"),
             )
 
+        def token_columns(first, tiles):
+            q, t = divmod(first, QUAD)
+            return q, slice(t * P, (t + tiles) * P)
+
         def x_quantise(j):
+            q, toks = token_columns(2 * j, 2)
             nc.vector.quantize_mx(
-                out=x_codes[j][:].bitcast(FP8X4),
-                scales=x_scales[j][:],
+                out=x_codes[q][:, toks].bitcast(FP8X4),
+                scales=x_scales[q][:, toks],
                 in_=x_grouped[j][:].rearrange("p h r t -> p (h r t)"),
             )
             ready.add(("x", j))
@@ -184,151 +203,271 @@ def tile_avey_pa_kernel(tc, x, g, W1, b1, out_0, out_1, out_2):
 
         enriched = {}
         accs = {}
+        mids = {}
 
-        def matmul(j, b):
-            accs[j, b] = []
-            for c in range(0, GROUPS, 2):
-                acc = psum_acc.tile([P, 2, 2 * P], F32, tag="acc", name="acc")
-                for h in range(2):
-                    feats = slice((c + h) * P, (c + h + 1) * P)
-                    nc.tensor.matmul_mx(
-                        out=acc[:, h, :],
-                        lhsT=w_codes[b][:, feats].bitcast(FP8X4),
-                        lhsT_scale=w_scales[b][:, feats],
-                        rhs=x_codes[j][:].bitcast(FP8X4),
-                        rhs_scale=x_scales[j][:],
-                        start=True,
-                        stop=True,
+        def matmul(share):
+            accs[share] = acc = psum_acc.tile([P, BANK], F32, tag="acc", name="acc")
+            if len(share) == 1:
+                q, toks = token_columns(share[0], 1)
+                nc.tensor.matmul_mx(
+                    out=acc[:],
+                    lhsT=x_codes[q][:, toks].bitcast(FP8X4),
+                    lhsT_scale=x_scales[q][:, toks],
+                    rhs=w_codes[H1][:].bitcast(FP8X4),
+                    rhs_scale=w_scales[H1][:],
+                    start=True,
+                    stop=True,
+                )
+                return
+            first, tiles, b, c = share
+            q, toks = token_columns(first, tiles)
+            for n in range(QUAD // tiles):
+                feats = slice((c + n) * P, (c + n + 1) * P)
+                nc.tensor.matmul_mx(
+                    out=acc[:, n * tiles * P : (n + 1) * tiles * P],
+                    lhsT=w_codes[b][:, feats].bitcast(FP8X4),
+                    lhsT_scale=w_scales[b][:, feats],
+                    rhs=x_codes[q][:, toks].bitcast(FP8X4),
+                    rhs_scale=x_scales[q][:, toks],
+                    start=True,
+                    stop=True,
+                )
+
+        def drain(share, engine):
+            acc = accs[share]
+            if len(share) == 1:
+                mids[share] = mid = tokens.tile([P, BANK], F32, name="mid")
+                nc.vector.tensor_tensor(out=mid[:], in0=acc[:], in1=token_bias[:], op=ALU.add)
+                return
+            first, tiles, b, c = share
+            mids[share] = mid = flip.tile([P, BANK], F32, name="flat")
+            for n in range(QUAD // tiles):
+                part = slice(n * tiles * P, (n + 1) * tiles * P)
+                if engine == "S":
+                    nc.scalar.activation(
+                        out=mid[:, part], in_=acc[:, part], func=ACT.Relu, bias=bias[:, c + n, b : b + 1]
                     )
-                accs[j, b].append(acc)
-
-        def work(j, b):
-            flats = []
-            for n, acc in enumerate(accs[j, b]):
-                flat = flip.tile([P, 2, 2 * P], F32, name="flat")
-                for h in range(2):
+                else:
                     nc.vector.tensor_scalar(
-                        out=flat[:, h, :],
-                        in0=acc[:, h, :],
-                        scalar1=bias[:, 2 * n + h, b : b + 1],
+                        out=mid[:, part],
+                        in0=acc[:, part],
+                        scalar1=bias[:, c + n, b : b + 1],
                         scalar2=0.0,
                         op0=ALU.add,
                         op1=ALU.max,
                     )
-                flats.append(flat)
-            enriched[j, b] = keep.tile([P, 2, BANK], F32, name="enriched%d%d" % (j, b))
-            for n, flat in enumerate(flats):
-                turned = psum_turn.tile([P, 2, 2, P], F32, tag="turn", name="turn")
-                for h in range(2):
-                    for i in range(2):
-                        nc.tensor.transpose(turned[:, i, h, :], flat[:, h, i * P : (i + 1) * P], ident_f32[:])
-                nc.scalar.activation(
-                    out=enriched[j, b][:, :, 2 * n * P : 2 * (n + 1) * P],
-                    in_=turned[:].rearrange("p i h r -> p i (h r)"),
-                    func=ACT.Square,
-                )
 
-        def store(j, b):
-            rows, first = outputs[b]
-            nc.sync.dma_start(
-                out=rows[:, 2 * j : 2 * j + 2, first : first + BANK], in_=enriched[j, b][:]
+        def finish(share):
+            mid = mids[share]
+            if len(share) == 1:
+                i = share[0]
+                if i % 2 == 0:
+                    enriched[i, H1] = keep.tile([P, 2, BANK], F32, name="enriched_h1_%d" % i)
+                result = enriched[i - i % 2, H1]
+                if i in LAST_TOKENS:
+                    nc.vector.scalar_tensor_tensor(
+                        out=result[:, i % 2, :], in0=mid[:], scalar=0.0, in1=mid[:], op0=ALU.max, op1=ALU.mult
+                    )
+                    return
+                above = tokens.tile([P, BANK], F32, name="above")
+                nc.gpsimd.tensor_scalar(
+                    out=above[:], in0=mid[:], scalar1=FLT_MAX, scalar2=0.0, op0=ALU.min, op1=ALU.max
+                )
+                nc.gpsimd.tensor_tensor(out=result[:, i % 2, :], in0=above[:], in1=above[:], op=ALU.mult)
+                return
+            first, tiles, b, c = share
+            if c == 0:
+                enriched[first, b] = keep.tile([P, tiles, BANK], F32, name="enriched%d%d" % (first, b))
+            width = QUAD // tiles
+            turned = psum_turn.tile([P, tiles, width, P], F32, tag="turn", name="turn")
+            for n in range(width):
+                for i in range(tiles):
+                    tok = slice((n * tiles + i) * P, (n * tiles + i + 1) * P)
+                    nc.tensor.transpose(turned[:, i, n, :], mid[:, tok], ident_f32[:])
+            nc.scalar.activation(
+                out=enriched[first, b][:, :, c * P : (c + width) * P],
+                in_=turned[:].rearrange("p i n r -> p i (n r)"),
+                func=ACT.Square,
             )
 
-        norm2 = [keep.tile([P, 2], F32, name="norm2_%d" % j) for j in range(PAIRS)]
-
-        def right_sums(j):
-            fourth = stage.tile([P, 2, HALF], BF16, name="fourth")
-            for i in range(2):
-                nc.scalar.activation(
-                    out=fourth[:, i, :],
-                    in_=enriched[j, RIGHT][:, i, :],
-                    func=ACT.Square,
-                    accum_out=norm2[j][:, i : i + 1],
+        def store(first, tiles, b):
+            rows, left = outputs[b]
+            for i in range(0, tiles, 2):
+                nc.sync.dma_start(
+                    out=rows[:, first + i : first + i + 2, left : left + BANK],
+                    in_=enriched[first, b][:, i : i + 2, :],
                 )
 
-        def right_scale(j):
+
+        inv_norm = {}
+
+        norm2 = {QUAD * q: keep.tile([P, QUAD], F32, name="norm2_%d" % q) for q in range(2)}
+
+        def right_sums_on_vector(first, *tiles):
+            fourth = stage.tile([P, HALF], BF16, name="fourth_v")
+            for i in tiles:
+                nc.vector.scalar_tensor_tensor(
+                    out=fourth[:],
+                    in0=enriched[first, RIGHT][:, i, :],
+                    scalar=1.0,
+                    in1=enriched[first, RIGHT][:, i, :],
+                    op0=ALU.mult,
+                    op1=ALU.mult,
+                    accum_out=norm2[first][:, i : i + 1],
+                )
+
+        def right_sums(first, *tiles):
+            fourth = stage.tile([P, HALF], BF16, name="fourth")
+            for i in tiles:
+                nc.scalar.activation(
+                    out=fourth[:],
+                    in_=enriched[first, RIGHT][:, i, :],
+                    func=ACT.Square,
+                    accum_out=norm2[first][:, i : i + 1],
+                )
+
+        def right_norms(first):
             floor = EPS_NORM * EPS_NORM
-            above = stage.tile([P, 2], F32, name="above")
-            nc.scalar.activation(out=above[:], in_=norm2[j][:], func=ACT.Relu, bias=-floor)
-            inv_norm = stage.tile([P, 2], F32, name="inv_norm")
-            nc.scalar.activation(out=inv_norm[:], in_=above[:], func=ACT.Abs_reciprocal_sqrt, bias=floor)
+            over = keep.tile([P, QUAD], F32, name="over%d" % first)
+            nc.scalar.activation(out=over[:], in_=norm2[first][:], func=ACT.Relu, bias=-floor)
+            inv_norm[first] = keep.tile([P, QUAD], F32, name="inv_norm%d" % first)
+            nc.scalar.activation(out=inv_norm[first][:], in_=over[:], func=ACT.Abs_reciprocal_sqrt, bias=floor)
+
+        def right_scale(first, t0, engine=nc.gpsimd):
+            unit_rows = keep.tile([P, 2, HALF], F32, name="unit_rows%d" % (first + t0))
             for i in range(2):
-                unit_rows = keep.tile([P, HALF], F32, name="unit_rows%d%d" % (j, i))
-                nc.gpsimd.tensor_scalar(
-                    out=unit_rows[:],
-                    in0=enriched[j, RIGHT][:, i, :],
-                    scalar1=inv_norm[:, i : i + 1],
+                engine.tensor_scalar(
+                    out=unit_rows[:, i, :],
+                    in0=enriched[first, RIGHT][:, t0 + i, :],
+                    scalar1=inv_norm[first][:, t0 + i : t0 + i + 1],
                     scalar2=1.0,
                     op0=ALU.mult,
                     op1=ALU.mult,
                 )
-                nc.sync.dma_start(out=right_rows[:, 2 * j + i, :], in_=unit_rows[:])
+            enriched[first + t0, UNIT] = unit_rows
 
         V = nc.vector.tensor_copy
-        S = nc.scalar.copy
+
+        def pair(j, b):
+            return (2 * j, 2, b, 0), (2 * j, 2, b, 2)
+
+        def quad(first, b, c):
+            return (first, 4, b, c), (first, 4, b, c + 1)
+
+        def multiply(shares):
+            for share in shares:
+                matmul(share)
+
+        def read(shares, engine="V"):
+            for share in shares:
+                drain(share, engine)
+
+        def end(shares):
+            for share in shares:
+                finish(share)
+
         x_stats(0, vector_half=True)
-        spread_gain()
-        turn_bias()
-        w_group(LEFT, S, BANK // 2, BANK)
-        x_turn(0)
-        w_group(LEFT, V, 0, BANK // 2)
+        spread_gain = spread(GAIN_ROW)
+        turned_bias = turn_bias()
+        spread_b1 = spread(H1)
+        V(out=gain[:], in_=spread_gain[:])
         x_stats(1)
+        x_norm(0)
+        V(out=bias[:], in_=turned_bias[:, :, 0:BANKS])
+        x_turn(0)
+        x_copy(0)
+        w_group(LEFT, V)
+        V(out=token_bias[:], in_=spread_b1[:])
+        x_stats(2)
         x_quantise(0)
         w_quantise(LEFT)
-        steps = [
-            (x_turn, 1),
-            (0, LEFT),
-            (w_group, RIGHT, S, BANK // 2, BANK),
-            (w_group, RIGHT, V, 0, BANK // 2),
-            (x_quantise, 1),
-            (x_stats, 2),
-            (1, LEFT),
-            (w_quantise, RIGHT),
-            (x_stats, 3),
-            (w_group, H0, V),
-            (0, RIGHT),
-            (x_turn, 2),
-            (1, RIGHT),
-            (w_quantise, H0),
-            (right_sums, 0),
-            (x_quantise, 2),
-            (0, H0),
-            (right_scale, 0),
-            (right_sums, 1),
-            (x_turn, 3),
-            (1, H0),
-            (right_scale, 1),
-            (2, LEFT),
-            (w_group, H1, V),
-            (x_quantise, 3),
-            (2, RIGHT),
-            (w_quantise, H1),
-            (2, H0),
-            (right_sums, 2),
-            (3, RIGHT),
-            (right_scale, 2),
-            (0, H1),
-            (right_sums, 3),
-            (1, H1),
-            (right_scale, 3),
-            (2, H1),
-            (3, H0),
-            (3, H1),
-            (3, LEFT),
-        ]
-        groups = [step for step in steps if isinstance(step[0], int)]
-        issued = worked = 0
-        for step in steps:
-            while issued < min(worked + LEAD + 1, len(groups)) and {
-                ("x", groups[issued][0]),
-                ("w", groups[issued][1]),
-            } <= ready:
-                matmul(*groups[issued])
-                issued += 1
-            if isinstance(step[0], int):
-                work(*step)
-                worked += 1
-                if step[1] != RIGHT:
-                    store(*step)
-            else:
-                step[0](*step[1:])
+        multiply(pair(0, LEFT))
+        x_norm(1)
+        read(pair(0, LEFT))
+        x_turn(1)
+        x_copy(1)
+        end(pair(0, LEFT))
+        store(0, 2, LEFT)
+        w_group(H0, V)
+        x_quantise(1)
+        w_quantise(H0)
+        multiply(pair(1, LEFT))
+        multiply(quad(0, H0, 0))
+        x_stats(3)
+        read(pair(1, LEFT), "S")
+        x_norm(2)
+        end(pair(1, LEFT))
+        store(2, 2, LEFT)
+        x_turn(2)
+        read(quad(0, H0, 0))
+        multiply(quad(0, H0, 2))
+        x_copy(2)
+        x_norm(3)
+        end(quad(0, H0, 0))
+        x_turn(3)
+        read(quad(0, H0, 2))
+        x_copy(3)
+        w_group(RIGHT, V)
+        end(quad(0, H0, 2))
+        store(0, 4, H0)
+        x_quantise(2)
+        x_quantise(3)
+        w_quantise(RIGHT)
+        multiply(quad(0, RIGHT, 0))
+        multiply(quad(0, RIGHT, 2))
+        read(quad(0, RIGHT, 0), "S")
+        w_group(H1, V)
+        end(quad(0, RIGHT, 0))
+        read(quad(0, RIGHT, 2))
+        multiply(quad(4, LEFT, 0))
+        end(quad(0, RIGHT, 2))
+        w_quantise(H1)
+        read(quad(4, LEFT, 0))
+        multiply(quad(4, LEFT, 2))
+        end(quad(4, LEFT, 0))
+        read(quad(4, LEFT, 2))
+        right_sums(0, 0, 1)
+        multiply(((4,), (5,)))
+        end(quad(4, LEFT, 2))
+        store(4, 4, LEFT)
+        right_sums(0, 2, 3)
+        right_norms(0)
+        read(((4,), (5,)))
+        multiply(quad(4, RIGHT, 0))
+        end(((4,), (5,)))
+        store(4, 2, H1)
+        read(quad(4, RIGHT, 0))
+        right_scale(0, 0)
+        right_scale(0, 2)
+        store(0, 2, UNIT)
+        store(2, 2, UNIT)
+        multiply(quad(4, RIGHT, 2))
+        end(quad(4, RIGHT, 0))
+        read(quad(4, RIGHT, 2))
+        multiply(((6,), (7,)))
+        end(quad(4, RIGHT, 2))
+        read(((6,), (7,)))
+        multiply(quad(0, H1, 0))
+        end(((6,), (7,)))
+        store(6, 2, H1)
+        right_sums(4, 0, 1)
+        read(quad(0, H1, 0))
+        right_sums(4, 2, 3)
+        right_norms(4)
+        multiply(quad(0, H1, 2))
+        end(quad(0, H1, 0))
+        read(quad(0, H1, 2))
+        multiply(pair(2, H0))
+        end(quad(0, H1, 2))
+        right_scale(4, 0, nc.vector)
+        right_scale(4, 2, nc.vector)
+        store(4, 2, UNIT)
+        store(6, 2, UNIT)
+        store(0, 4, H1)
+        multiply(pair(3, H0))
+        read(pair(2, H0))
+        end(pair(2, H0))
+        store(4, 2, H0)
+        read(pair(3, H0))
+        end(pair(3, H0))
+        store(6, 2, H0)

@@ -377,50 +377,50 @@ def tile_avey_pa_kernel(tc, x, g, W1, b1, out_0, out_1, out_2):
         x_turn(0)
         x_copy(0)
         w_group(LEFT, V)
-        V(out=token_bias[:], in_=spread_b1[:])
         x_stats(2)
+        x_norm(1)
+        x_turn(1)
         x_quantise(0)
         w_quantise(LEFT)
-        multiply(pair(0, LEFT))
-        x_norm(1)
-        read(pair(0, LEFT))
-        x_turn(1)
+        V(out=token_bias[:], in_=spread_b1[:])
         x_copy(1)
+        multiply(pair(0, LEFT))
+        read(pair(0, LEFT), "S")
+        w_group(H0, V)
+        x_stats(3)
         end(pair(0, LEFT))
         store(0, 2, LEFT)
-        w_group(H0, V)
         x_quantise(1)
         w_quantise(H0)
         multiply(pair(1, LEFT))
         multiply(quad(0, H0, 0))
-        x_stats(3)
-        read(pair(1, LEFT), "S")
         x_norm(2)
+        read(pair(1, LEFT))
         end(pair(1, LEFT))
         store(2, 2, LEFT)
         x_turn(2)
         read(quad(0, H0, 0))
         multiply(quad(0, H0, 2))
         x_copy(2)
-        x_norm(3)
-        end(quad(0, H0, 0))
-        x_turn(3)
-        read(quad(0, H0, 2))
-        x_copy(3)
         w_group(RIGHT, V)
+        end(quad(0, H0, 0))
+        read(quad(0, H0, 2))
+        w_quantise(RIGHT)
+        x_norm(3)
         end(quad(0, H0, 2))
         store(0, 4, H0)
-        x_quantise(2)
-        x_quantise(3)
-        w_quantise(RIGHT)
         multiply(quad(0, RIGHT, 0))
         multiply(quad(0, RIGHT, 2))
+        x_turn(3)
         read(quad(0, RIGHT, 0), "S")
-        w_group(H1, V)
+        x_quantise(2)
+        x_copy(3)
         end(quad(0, RIGHT, 0))
         read(quad(0, RIGHT, 2))
-        multiply(quad(4, LEFT, 0))
+        w_group(H1, V)
+        x_quantise(3)
         end(quad(0, RIGHT, 2))
+        multiply(quad(4, LEFT, 0))
         w_quantise(H1)
         read(quad(4, LEFT, 0))
         multiply(quad(4, LEFT, 2))

@@ -52,7 +52,7 @@ def tile_avey_pa_kernel(tc, x, g, W1, b1, out_0, out_1, out_2):
     with ExitStack() as ctx:
         keep = ctx.enter_context(tc.tile_pool(name="keep", bufs=1))
         stage = ctx.enter_context(tc.tile_pool(name="stage", bufs=2))
-        flip = ctx.enter_context(tc.tile_pool(name="flip", bufs=4))
+        flip = ctx.enter_context(tc.tile_pool(name="flip", bufs=6))
         tokens = ctx.enter_context(tc.tile_pool(name="tokens", bufs=3))
         psum_turn = ctx.enter_context(tc.psum_pool(name="psum_turn", bufs=4))
         psum_acc = ctx.enter_context(tc.psum_pool(name="psum_acc", bufs=4))
@@ -80,9 +80,9 @@ def tile_avey_pa_kernel(tc, x, g, W1, b1, out_0, out_1, out_2):
         load_x(1)
         load_w(H0)
         load_x(2)
-        load_w(RIGHT)
-        load_x(3)
         load_w(H1)
+        load_x(3)
+        load_w(RIGHT)
 
         ident = keep.tile([P, P], BF16)
         masks.make_identity(nc, ident[:])
@@ -192,6 +192,20 @@ def tile_avey_pa_kernel(tc, x, g, W1, b1, out_0, out_1, out_2):
                 out=w_grouped[b][:, first:last, :].rearrange("p (c i) t -> p c t i", i=4),
                 in_=w_raw[b][:, :, first:last].rearrange("p t (c i) -> p c t i", i=4),
             )
+
+        def w_group_gpsimd(b):
+            go = keep.tile([P, 1], F32, name="go%d" % b)
+            nc.vector.memset(go[:], 1.0)
+            for half in range(2):
+                here = slice(half * 2 * P, (half + 1) * 2 * P)
+                nc.gpsimd.tensor_scalar(
+                    out=w_grouped[b][:, here, :],
+                    in0=w_raw[b][:, :, here].rearrange("p t f -> p f t"),
+                    scalar1=go[:, 0:1],
+                    scalar2=1.0,
+                    op0=ALU.mult,
+                    op1=ALU.mult,
+                )
 
         def w_quantise(b):
             nc.vector.quantize_mx(
@@ -395,6 +409,7 @@ def tile_avey_pa_kernel(tc, x, g, W1, b1, out_0, out_1, out_2):
         multiply(pair(1, LEFT))
         multiply(quad(0, H0, 0))
         x_norm(2)
+        w_group_gpsimd(H1)
         read(pair(1, LEFT))
         end(pair(1, LEFT))
         store(2, 2, LEFT)
@@ -402,72 +417,72 @@ def tile_avey_pa_kernel(tc, x, g, W1, b1, out_0, out_1, out_2):
         read(quad(0, H0, 0))
         multiply(quad(0, H0, 2))
         x_copy(2)
-        w_group(RIGHT, V)
         end(quad(0, H0, 0))
         read(quad(0, H0, 2))
-        w_quantise(RIGHT)
-        x_norm(3)
+        x_quantise(2)
+        w_quantise(H1)
         end(quad(0, H0, 2))
         store(0, 4, H0)
-        multiply(quad(0, RIGHT, 0))
-        multiply(quad(0, RIGHT, 2))
+        multiply(pair(2, LEFT))
+        multiply(quad(0, H1, 0))
+        x_norm(3)
         x_turn(3)
-        read(quad(0, RIGHT, 0), "S")
-        x_quantise(2)
+        read(pair(2, LEFT), "S")
         x_copy(3)
+        read(quad(0, H1, 0))
+        end(pair(2, LEFT))
+        store(4, 2, LEFT)
+        multiply(quad(0, H1, 2))
+        end(quad(0, H1, 0))
+        w_group(RIGHT, V)
+        read(quad(0, H1, 2))
+        x_quantise(3)
+        end(quad(0, H1, 2))
+        store(0, 4, H1)
+        multiply(pair(3, LEFT))
+        w_quantise(RIGHT)
+        read(pair(3, LEFT))
+        multiply(quad(0, RIGHT, 0))
+        end(pair(3, LEFT))
+        store(6, 2, LEFT)
+        read(quad(0, RIGHT, 0))
+        multiply(quad(0, RIGHT, 2))
         end(quad(0, RIGHT, 0))
         read(quad(0, RIGHT, 2))
-        w_group(H1, V)
-        x_quantise(3)
-        end(quad(0, RIGHT, 2))
-        multiply(quad(4, LEFT, 0))
-        w_quantise(H1)
-        read(quad(4, LEFT, 0))
-        multiply(quad(4, LEFT, 2))
-        end(quad(4, LEFT, 0))
-        read(quad(4, LEFT, 2))
-        right_sums(0, 0, 1)
-        multiply(((4,), (5,)))
-        end(quad(4, LEFT, 2))
-        store(4, 4, LEFT)
-        right_sums(0, 2, 3)
-        right_norms(0)
-        read(((4,), (5,)))
         multiply(quad(4, RIGHT, 0))
+        end(quad(0, RIGHT, 2))
+        read(quad(4, RIGHT, 0))
+        multiply(((4,), (5,)))
+        right_sums(0, 0, 1)
+        read(((4,), (5,)))
+        multiply(((6,), (7,)))
         end(((4,), (5,)))
         store(4, 2, H1)
-        read(quad(4, RIGHT, 0))
+        right_sums(0, 2, 3)
+        right_norms(0)
+        end(quad(4, RIGHT, 0))
+        multiply(quad(4, RIGHT, 2))
+        read(((6,), (7,)))
+        read(quad(4, RIGHT, 2))
+        end(((6,), (7,)))
+        store(6, 2, H1)
         right_scale(0, 0)
         right_scale(0, 2)
         store(0, 2, UNIT)
         store(2, 2, UNIT)
-        multiply(quad(4, RIGHT, 2))
-        end(quad(4, RIGHT, 0))
-        read(quad(4, RIGHT, 2))
-        multiply(((6,), (7,)))
-        end(quad(4, RIGHT, 2))
-        read(((6,), (7,)))
-        multiply(quad(0, H1, 0))
-        end(((6,), (7,)))
-        store(6, 2, H1)
-        right_sums(4, 0, 1)
-        read(quad(0, H1, 0))
-        right_sums(4, 2, 3)
-        right_norms(4)
-        multiply(quad(0, H1, 2))
-        end(quad(0, H1, 0))
-        read(quad(0, H1, 2))
         multiply(pair(2, H0))
-        end(quad(0, H1, 2))
+        end(quad(4, RIGHT, 2))
+        read(pair(2, H0))
+        multiply(pair(3, H0))
+        right_sums(4, 0, 1)
+        end(pair(2, H0))
+        right_sums_on_vector(4, 2, 3)
+        right_norms(4)
+        read(pair(3, H0))
         right_scale(4, 0, nc.vector)
         right_scale(4, 2, nc.vector)
+        store(4, 2, H0)
         store(4, 2, UNIT)
         store(6, 2, UNIT)
-        store(0, 4, H1)
-        multiply(pair(3, H0))
-        read(pair(2, H0))
-        end(pair(2, H0))
-        store(4, 2, H0)
-        read(pair(3, H0))
         end(pair(3, H0))
         store(6, 2, H0)

@@ -76,12 +76,12 @@ def tile_avey_pa_kernel(tc, x, g, W1, b1, out_0, out_1, out_2):
         load_x(0)
         nc.sync.dma_start(out=consts[GAIN_ROW : GAIN_ROW + 1, :], in_=g.unsqueeze(0))
         nc.sync.dma_start(out=consts[0:BANKS, :], in_=b1.rearrange("(r c) -> r c", c=BANK))
-        load_w(LEFT)
         load_x(1)
-        load_w(H0)
+        load_w(LEFT)
         load_x(2)
-        load_w(H1)
+        load_w(H0)
         load_x(3)
+        load_w(H1)
         load_w(RIGHT)
 
         ident = keep.tile([P, P], BF16)
@@ -449,23 +449,23 @@ def tile_avey_pa_kernel(tc, x, g, W1, b1, out_0, out_1, out_2):
         multiply(quad(0, RIGHT, 2))
         end(quad(0, RIGHT, 0))
         read(quad(0, RIGHT, 2))
-        multiply(quad(4, RIGHT, 0))
-        end(quad(0, RIGHT, 2))
-        read(quad(4, RIGHT, 0))
         multiply(((4,), (5,)))
-        right_sums(0, 0, 1)
+        end(quad(0, RIGHT, 2))
         read(((4,), (5,)))
-        multiply(((6,), (7,)))
+        multiply(quad(4, RIGHT, 0))
+        right_sums(0, 0, 1)
         end(((4,), (5,)))
         store(4, 2, H1)
+        read(quad(4, RIGHT, 0))
+        multiply(((6,), (7,)))
         right_sums(0, 2, 3)
         right_norms(0)
         end(quad(4, RIGHT, 0))
         multiply(quad(4, RIGHT, 2))
         read(((6,), (7,)))
-        read(quad(4, RIGHT, 2))
         end(((6,), (7,)))
         store(6, 2, H1)
+        read(quad(4, RIGHT, 2))
         right_scale(0, 0)
         right_scale(0, 2)
         store(0, 2, UNIT)
@@ -474,15 +474,15 @@ def tile_avey_pa_kernel(tc, x, g, W1, b1, out_0, out_1, out_2):
         end(quad(4, RIGHT, 2))
         read(pair(2, H0))
         multiply(pair(3, H0))
-        right_sums(4, 0, 1)
         end(pair(2, H0))
-        right_sums_on_vector(4, 2, 3)
-        right_norms(4)
-        read(pair(3, H0))
-        right_scale(4, 0, nc.vector)
-        right_scale(4, 2, nc.vector)
         store(4, 2, H0)
-        store(4, 2, UNIT)
-        store(6, 2, UNIT)
+        read(pair(3, H0))
+        right_sums_on_vector(4, 1, 2, 3)
         end(pair(3, H0))
         store(6, 2, H0)
+        right_sums(4, 0)
+        right_norms(4)
+        right_scale(4, 0, nc.vector)
+        right_scale(4, 2, nc.vector)
+        store(4, 2, UNIT)
+        store(6, 2, UNIT)

@@ -20,7 +20,7 @@ HALF = 512
 E = HEAD + HALF + HALF
 BANK = 512
 TOK_TILES = TOKENS // P
-LAST_TOKENS = (4, 5, 6, 7)
+GPSIMD_TOKENS = (0, 1, 2, 3)
 FLT_MAX = 3.4028234663852886e38
 PAIRS = TOK_TILES // 2
 QUAD = 4
@@ -51,10 +51,11 @@ def tile_avey_pa_kernel(tc, x, g, W1, b1, out_0, out_1, out_2):
 
     with ExitStack() as ctx:
         keep = ctx.enter_context(tc.tile_pool(name="keep", bufs=1))
-        stage = ctx.enter_context(tc.tile_pool(name="stage", bufs=2))
+        stage = ctx.enter_context(tc.tile_pool(name="stage", bufs=3))
         flip = ctx.enter_context(tc.tile_pool(name="flip", bufs=6))
-        tokens = ctx.enter_context(tc.tile_pool(name="tokens", bufs=3))
-        psum_turn = ctx.enter_context(tc.psum_pool(name="psum_turn", bufs=4))
+        tokens = ctx.enter_context(tc.tile_pool(name="tokens", bufs=6))
+        psum_gain = ctx.enter_context(tc.psum_pool(name="psum_gain", bufs=1))
+        psum_turn = ctx.enter_context(tc.psum_pool(name="psum_turn", bufs=3))
         psum_acc = ctx.enter_context(tc.psum_pool(name="psum_acc", bufs=4))
         ctx.enter_context(tc.manual_schedule())
 
@@ -79,23 +80,22 @@ def tile_avey_pa_kernel(tc, x, g, W1, b1, out_0, out_1, out_2):
         load_x(1)
         load_w(LEFT)
         load_x(2)
-        load_w(H0)
-        load_x(3)
-        load_w(H1)
         load_w(RIGHT)
+        load_x(3)
+        load_w(H0)
+        load_w(H1)
 
         ident = keep.tile([P, P], BF16)
         masks.make_identity(nc, ident[:])
         ident_f32 = keep.tile([P, P], F32)
         masks.make_identity(nc, ident_f32[:])
 
-        gain = keep.tile([P, D], BF16)
+        gain = psum_gain.tile([P, D], BF16)
         bias = keep.tile([P, GROUPS, BANKS], F32)
 
         token_bias = keep.tile([P, BANK], BF16)
 
-        def spread(row):
-            acc = psum_acc.tile([P, BANK], BF16, tag="acc", name="acc")
+        def spread(row, acc):
             nc.tensor.matmul(
                 out=acc[:],
                 lhsT=ident[:, row : row + 1].to_broadcast([P, P]),
@@ -103,7 +103,6 @@ def tile_avey_pa_kernel(tc, x, g, W1, b1, out_0, out_1, out_2):
                 start=True,
                 stop=True,
             )
-            return acc
 
         def turn_bias():
             turned = psum_turn.tile([P, GROUPS, P], BF16, tag="turn", name="turn")
@@ -193,11 +192,11 @@ def tile_avey_pa_kernel(tc, x, g, W1, b1, out_0, out_1, out_2):
                 in_=w_raw[b][:, :, first:last].rearrange("p t (c i) -> p c t i", i=4),
             )
 
-        def w_group_gpsimd(b):
+        def w_group_gpsimd(b, wait=True):
             go = keep.tile([P, 1], F32, name="go%d" % b)
             nc.vector.memset(go[:], 1.0)
-            for half in range(2):
-                here = slice(half * 2 * P, (half + 1) * 2 * P)
+            for part in range(GROUPS):
+                here = slice(part * P, (part + 1) * P)
                 nc.gpsimd.tensor_scalar(
                     out=w_grouped[b][:, here, :],
                     in0=w_raw[b][:, :, here].rearrange("p t f -> p f t"),
@@ -278,7 +277,7 @@ def tile_avey_pa_kernel(tc, x, g, W1, b1, out_0, out_1, out_2):
                 if i % 2 == 0:
                     enriched[i, H1] = keep.tile([P, 2, BANK], F32, name="enriched_h1_%d" % i)
                 result = enriched[i - i % 2, H1]
-                if i in LAST_TOKENS:
+                if i not in GPSIMD_TOKENS:
                     nc.vector.scalar_tensor_tensor(
                         out=result[:, i % 2, :], in0=mid[:], scalar=0.0, in1=mid[:], op0=ALU.max, op1=ALU.mult
                     )
@@ -313,52 +312,44 @@ def tile_avey_pa_kernel(tc, x, g, W1, b1, out_0, out_1, out_2):
                 )
 
 
-        inv_norm = {}
+        norm2 = [keep.tile([P, 2], F32, name="norm2_%d" % j) for j in range(PAIRS)]
+        inv_norm = [keep.tile([P, 2], F32, name="inv_norm%d" % j) for j in range(PAIRS)]
 
-        norm2 = {QUAD * q: keep.tile([P, QUAD], F32, name="norm2_%d" % q) for q in range(2)}
-
-        def right_sums_on_vector(first, *tiles):
-            fourth = stage.tile([P, HALF], BF16, name="fourth_v")
-            for i in tiles:
+        def right_sum(j, i, engine="S"):
+            rows = enriched[2 * j, RIGHT][:, i, :]
+            fourth = stage.tile([P, HALF], BF16, name="fourth" + engine)
+            if engine == "S":
+                nc.scalar.activation(out=fourth[:], in_=rows, func=ACT.Square, accum_out=norm2[j][:, i : i + 1])
+            else:
                 nc.vector.scalar_tensor_tensor(
                     out=fourth[:],
-                    in0=enriched[first, RIGHT][:, i, :],
+                    in0=rows,
                     scalar=1.0,
-                    in1=enriched[first, RIGHT][:, i, :],
+                    in1=rows,
                     op0=ALU.mult,
                     op1=ALU.mult,
-                    accum_out=norm2[first][:, i : i + 1],
+                    accum_out=norm2[j][:, i : i + 1],
                 )
 
-        def right_sums(first, *tiles):
-            fourth = stage.tile([P, HALF], BF16, name="fourth")
-            for i in tiles:
-                nc.scalar.activation(
-                    out=fourth[:],
-                    in_=enriched[first, RIGHT][:, i, :],
-                    func=ACT.Square,
-                    accum_out=norm2[first][:, i : i + 1],
-                )
-
-        def right_norms(first):
+        def right_norm(j):
             floor = EPS_NORM * EPS_NORM
-            over = keep.tile([P, QUAD], F32, name="over%d" % first)
-            nc.scalar.activation(out=over[:], in_=norm2[first][:], func=ACT.Relu, bias=-floor)
-            inv_norm[first] = keep.tile([P, QUAD], F32, name="inv_norm%d" % first)
-            nc.scalar.activation(out=inv_norm[first][:], in_=over[:], func=ACT.Abs_reciprocal_sqrt, bias=floor)
+            over = stage.tile([P, 2], F32, name="over")
+            nc.scalar.activation(out=over[:], in_=norm2[j][:], func=ACT.Relu, bias=-floor)
+            nc.scalar.activation(out=inv_norm[j][:], in_=over[:], func=ACT.Abs_reciprocal_sqrt, bias=floor)
 
-        def right_scale(first, t0, engine=nc.gpsimd):
-            unit_rows = keep.tile([P, 2, HALF], F32, name="unit_rows%d" % (first + t0))
+        def right_scale(j, engine):
+            unit_rows = keep.tile([P, 2, HALF], F32, name="unit_rows%d" % j)
             for i in range(2):
                 engine.tensor_scalar(
                     out=unit_rows[:, i, :],
-                    in0=enriched[first, RIGHT][:, t0 + i, :],
-                    scalar1=inv_norm[first][:, t0 + i : t0 + i + 1],
+                    in0=enriched[2 * j, RIGHT][:, i, :],
+                    scalar1=inv_norm[j][:, i : i + 1],
                     scalar2=1.0,
                     op0=ALU.mult,
                     op1=ALU.mult,
                 )
-            enriched[first + t0, UNIT] = unit_rows
+            enriched[2 * j, UNIT] = unit_rows
+            store(2 * j, 2, UNIT)
 
         V = nc.vector.tensor_copy
 
@@ -381,10 +372,10 @@ def tile_avey_pa_kernel(tc, x, g, W1, b1, out_0, out_1, out_2):
                 finish(share)
 
         x_stats(0, vector_half=True)
-        spread_gain = spread(GAIN_ROW)
+        spread(GAIN_ROW, gain)
         turned_bias = turn_bias()
-        spread_b1 = spread(H1)
-        V(out=gain[:], in_=spread_gain[:])
+        spread_b1 = psum_acc.tile([P, BANK], BF16, tag="acc", name="acc")
+        spread(H1, spread_b1)
         x_stats(1)
         x_norm(0)
         V(out=bias[:], in_=turned_bias[:, :, 0:BANKS])
@@ -396,93 +387,101 @@ def tile_avey_pa_kernel(tc, x, g, W1, b1, out_0, out_1, out_2):
         x_turn(1)
         x_quantise(0)
         w_quantise(LEFT)
+        w_group_gpsimd(RIGHT)
         V(out=token_bias[:], in_=spread_b1[:])
-        x_copy(1)
-        multiply(pair(0, LEFT))
-        read(pair(0, LEFT), "S")
-        w_group(H0, V)
         x_stats(3)
-        end(pair(0, LEFT))
-        store(0, 2, LEFT)
-        x_quantise(1)
-        w_quantise(H0)
-        multiply(pair(1, LEFT))
-        multiply(quad(0, H0, 0))
+        x_copy(1)
+        l = [pair(j, LEFT) for j in range(PAIRS)]
+        h = [pair(j, H0) for j in range(PAIRS)]
+        r = [pair(j, RIGHT) for j in range(PAIRS)]
+        t = [((2 * j,), (2 * j + 1,)) for j in range(PAIRS)]
+        multiply(l[0])
         x_norm(2)
-        w_group_gpsimd(H1)
-        read(pair(1, LEFT))
-        end(pair(1, LEFT))
-        store(2, 2, LEFT)
         x_turn(2)
-        read(quad(0, H0, 0))
-        multiply(quad(0, H0, 2))
-        x_copy(2)
-        end(quad(0, H0, 0))
-        read(quad(0, H0, 2))
-        x_quantise(2)
-        w_quantise(H1)
-        end(quad(0, H0, 2))
-        store(0, 4, H0)
-        multiply(pair(2, LEFT))
-        multiply(quad(0, H1, 0))
+        read(l[0], "S")
         x_norm(3)
-        x_turn(3)
-        read(pair(2, LEFT), "S")
-        x_copy(3)
-        read(quad(0, H1, 0))
-        end(pair(2, LEFT))
-        store(4, 2, LEFT)
-        multiply(quad(0, H1, 2))
-        end(quad(0, H1, 0))
-        w_group(RIGHT, V)
-        read(quad(0, H1, 2))
-        x_quantise(3)
-        end(quad(0, H1, 2))
-        store(0, 4, H1)
-        multiply(pair(3, LEFT))
+        x_quantise(1)
         w_quantise(RIGHT)
-        read(pair(3, LEFT))
-        multiply(quad(0, RIGHT, 0))
-        end(pair(3, LEFT))
+        w_group_gpsimd(H0)
+        x_copy(2)
+        end(l[0])
+        store(0, 2, LEFT)
+        multiply(l[1])
+        x_turn(3)
+        multiply(r[0])
+        read(l[1])
+        x_copy(3)
+        end(l[1])
+        store(2, 2, LEFT)
+        read(r[0])
+        x_quantise(2)
+        w_group_gpsimd(H1)
+        end(r[0])
+        multiply(l[2])
+        multiply(r[1])
+        read(l[2])
+        right_sum(0, 0)
+        right_sum(0, 1)
+        right_norm(0)
+        end(l[2])
+        store(4, 2, LEFT)
+        x_quantise(3)
+        read(r[1])
+        multiply(l[3])
+        w_quantise(H0)
+        end(r[1])
+        right_scale(0, nc.vector)
+        read(l[3])
+        multiply(h[0])
+        w_quantise(H1)
+        end(l[3])
         store(6, 2, LEFT)
-        read(quad(0, RIGHT, 0))
-        multiply(quad(0, RIGHT, 2))
-        end(quad(0, RIGHT, 0))
-        read(quad(0, RIGHT, 2))
-        multiply(((4,), (5,)))
-        end(quad(0, RIGHT, 2))
-        read(((4,), (5,)))
-        multiply(quad(4, RIGHT, 0))
-        right_sums(0, 0, 1)
-        end(((4,), (5,)))
-        store(4, 2, H1)
-        read(quad(4, RIGHT, 0))
-        multiply(((6,), (7,)))
-        right_sums(0, 2, 3)
-        right_norms(0)
-        end(quad(4, RIGHT, 0))
-        multiply(quad(4, RIGHT, 2))
-        read(((6,), (7,)))
-        end(((6,), (7,)))
-        store(6, 2, H1)
-        read(quad(4, RIGHT, 2))
-        right_scale(0, 0)
-        right_scale(0, 2)
-        store(0, 2, UNIT)
-        store(2, 2, UNIT)
-        multiply(pair(2, H0))
-        end(quad(4, RIGHT, 2))
-        read(pair(2, H0))
-        multiply(pair(3, H0))
-        end(pair(2, H0))
+        multiply(t[0])
+        right_sum(1, 0)
+        read(h[0])
+        right_sum(1, 1)
+        right_norm(1)
+        read(t[0])
+        multiply(h[1])
+        end(h[0])
+        store(0, 2, H0)
+        multiply(r[2])
+        end(t[0])
+        read(h[1])
+        multiply(t[1])
+        end(h[1])
+        store(2, 2, H0)
+        store(0, 2, H1)
+        read(r[2])
+        right_scale(1, nc.vector)
+        multiply(r[3])
+        end(r[2])
+        read(t[1])
+        end(t[1])
+        store(2, 2, H1)
+        multiply(h[2])
+        read(r[3])
+        multiply(t[2])
+        end(r[3])
+        right_sum(2, 0)
+        right_sum(2, 1)
+        right_norm(2)
+        read(h[2])
+        multiply(h[3])
+        end(h[2])
         store(4, 2, H0)
-        read(pair(3, H0))
-        right_sums_on_vector(4, 1, 2, 3)
-        end(pair(3, H0))
+        read(t[2])
+        end(t[2])
+        store(4, 2, H1)
+        right_sum(3, 0)
+        right_sum(3, 1)
+        right_norm(3)
+        read(h[3])
+        multiply(t[3])
+        end(h[3])
+        right_scale(2, nc.vector)
         store(6, 2, H0)
-        right_sums(4, 0)
-        right_norms(4)
-        right_scale(4, 0, nc.vector)
-        right_scale(4, 2, nc.vector)
-        store(4, 2, UNIT)
-        store(6, 2, UNIT)
+        read(t[3])
+        right_scale(3, nc.vector)
+        end(t[3])
+        store(6, 2, H1)

@@ -59,11 +59,19 @@ def tile_avey_pa_kernel(tc, x, g, W1, b1, out_0, out_1, out_2):
         psum_acc = ctx.enter_context(tc.psum_pool(name="psum_acc", bufs=4))
         ctx.enter_context(tc.manual_schedule())
 
-        x_sb = [keep.tile([P, 2, D], BF16, name="x_sb%d" % j) for j in range(PAIRS)]
+        x_first = [keep.tile([P, 1, D], BF16, name="x_first%d" % i) for i in range(2)]
+        x_pairs = [keep.tile([P, 2, D], BF16, name="x_pair%d" % j) for j in range(1, PAIRS)]
+        x_sb = [x_first[0][:, 0, :], x_first[1][:, 0, :]]
+        for pair_tile in x_pairs:
+            x_sb += [pair_tile[:, 0, :], pair_tile[:, 1, :]]
         w_raw = [keep.tile([P, PACK, BANK], BF16, name="w_raw%d" % b) for b in range(BANKS)]
 
         def load_x(j):
-            nc.sync.dma_start(out=x_sb[j][:], in_=x_rows[:, 2 * j : 2 * j + 2, :])
+            if j == 0:
+                for i in range(2):
+                    nc.sync.dma_start(out=x_first[i][:], in_=x_rows[:, i : i + 1, :])
+                return
+            nc.sync.dma_start(out=x_pairs[j - 1][:], in_=x_rows[:, 2 * j : 2 * j + 2, :])
 
         def load_w(b):
             nc.sync.dma_start(out=w_raw[b][:], in_=w_rows[:, :, cols(b)])
@@ -90,7 +98,7 @@ def tile_avey_pa_kernel(tc, x, g, W1, b1, out_0, out_1, out_2):
         ident_f32 = keep.tile([P, P], F32)
         masks.make_identity(nc, ident_f32[:])
 
-        gain = psum_gain.tile([P, D], BF16)
+        gain = psum_gain.tile([P, D], BF16, tag="gain")
         bias = keep.tile([P, GROUPS, BANKS], F32)
 
         token_bias = keep.tile([P, BANK], BF16)
@@ -118,31 +126,38 @@ def tile_avey_pa_kernel(tc, x, g, W1, b1, out_0, out_1, out_2):
         w_scales = [keep.tile([P, BANK], U8, align_bytes=64, name="w_scales%d" % b) for b in range(BANKS)]
         x_grouped = [keep.tile([P, 2, P, PACK], BF16, align_bytes=64, name="x_grouped%d" % j) for j in range(PAIRS)]
         w_grouped = [keep.tile([P, BANK, PACK], BF16, align_bytes=64, name="w_grouped%d" % b) for b in range(BANKS)]
+        sumsq = [keep.tile([P, 2], F32, name="sumsq%d" % j) for j in range(PAIRS)]
         rstd = [keep.tile([P, 2], F32, name="rstd%d" % j) for j in range(PAIRS)]
 
-        def x_stats(j, vector_half=False):
-            squares = stage.tile([P, 2, D], BF16, name="squares")
-            sumsq = stage.tile([P, 2], F32, name="sumsq")
-            nc.scalar.activation(
-                out=squares[:, 0, :], in_=x_sb[j][:, 0, :], func=ACT.Square, accum_out=sumsq[:, 0:1]
-            )
-            if vector_half:
+        def x_square(i, engine="S"):
+            squares = stage.tile([P, D], BF16, name="squares" + engine)
+            total = sumsq[i // 2][:, i % 2 : i % 2 + 1]
+            if engine == "S":
+                nc.scalar.activation(out=squares[:], in_=x_sb[i], func=ACT.Square, accum_out=total)
+            else:
                 nc.vector.scalar_tensor_tensor(
-                    out=squares[:, 1, :],
-                    in0=x_sb[j][:, 1, :],
+                    out=squares[:],
+                    in0=x_sb[i],
                     scalar=1.0,
-                    in1=x_sb[j][:, 1, :],
+                    in1=x_sb[i],
                     op0=ALU.mult,
                     op1=ALU.mult,
-                    accum_out=sumsq[:, 1:2],
+                    accum_out=total,
                 )
-            else:
-                nc.scalar.activation(
-                    out=squares[:, 1, :], in_=x_sb[j][:, 1, :], func=ACT.Square, accum_out=sumsq[:, 1:2]
-                )
+
+        def x_rstd(j, here=slice(0, 2)):
             nc.scalar.activation(
-                out=rstd[j][:], in_=sumsq[:], func=ACT.Abs_reciprocal_sqrt, bias=EPS_RMS, scale=1.0 / D
+                out=rstd[j][:, here],
+                in_=sumsq[j][:, here],
+                func=ACT.Abs_reciprocal_sqrt,
+                bias=EPS_RMS,
+                scale=1.0 / D,
             )
+
+        def x_stats(j):
+            x_square(2 * j)
+            x_square(2 * j + 1)
+            x_rstd(j)
 
         xns = {}
         turneds = {}
@@ -152,7 +167,7 @@ def tile_avey_pa_kernel(tc, x, g, W1, b1, out_0, out_1, out_2):
             for h in range(2):
                 nc.vector.scalar_tensor_tensor(
                     out=xn[:, h, :],
-                    in0=x_sb[j][:, h, :],
+                    in0=x_sb[2 * j + h],
                     scalar=rstd[j][:, h : h + 1],
                     in1=gain[:],
                     op0=ALU.mult,
@@ -195,8 +210,8 @@ def tile_avey_pa_kernel(tc, x, g, W1, b1, out_0, out_1, out_2):
         def w_group_gpsimd(b, wait=True):
             go = keep.tile([P, 1], F32, name="go%d" % b)
             nc.vector.memset(go[:], 1.0)
-            for part in range(GROUPS):
-                here = slice(part * P, (part + 1) * P)
+            for half in range(2):
+                here = slice(half * 2 * P, (half + 1) * 2 * P)
                 nc.gpsimd.tensor_scalar(
                     out=w_grouped[b][:, here, :],
                     in0=w_raw[b][:, :, here].rearrange("p t f -> p f t"),
@@ -217,6 +232,7 @@ def tile_avey_pa_kernel(tc, x, g, W1, b1, out_0, out_1, out_2):
         enriched = {}
         accs = {}
         mids = {}
+        turns = []
 
         def matmul(share):
             accs[share] = acc = psum_acc.tile([P, BANK], F32, tag="acc", name="acc")
@@ -292,7 +308,9 @@ def tile_avey_pa_kernel(tc, x, g, W1, b1, out_0, out_1, out_2):
             if c == 0:
                 enriched[first, b] = keep.tile([P, tiles, BANK], F32, name="enriched%d%d" % (first, b))
             width = QUAD // tiles
-            turned = psum_turn.tile([P, tiles, width, P], F32, tag="turn", name="turn")
+            pool, tag = (psum_gain, "gain") if len(turns) % 4 == 3 else (psum_turn, "turn")
+            turns.append(share)
+            turned = pool.tile([P, tiles, width, P], F32, tag=tag, name="turn")
             for n in range(width):
                 for i in range(tiles):
                     tok = slice((n * tiles + i) * P, (n * tiles + i + 1) * P)
@@ -371,7 +389,10 @@ def tile_avey_pa_kernel(tc, x, g, W1, b1, out_0, out_1, out_2):
             for share in shares:
                 finish(share)
 
-        x_stats(0, vector_half=True)
+        x_square(0)
+        x_rstd(0, slice(0, 1))
+        x_square(1, "V")
+        x_rstd(0, slice(1, 2))
         spread(GAIN_ROW, gain)
         turned_bias = turn_bias()
         spread_b1 = psum_acc.tile([P, BANK], BF16, tag="acc", name="acc")
@@ -402,20 +423,20 @@ def tile_avey_pa_kernel(tc, x, g, W1, b1, out_0, out_1, out_2):
         x_norm(3)
         x_quantise(1)
         w_quantise(RIGHT)
-        w_group_gpsimd(H0)
         x_copy(2)
         end(l[0])
         store(0, 2, LEFT)
         multiply(l[1])
         x_turn(3)
+        w_group(H0, V)
+        w_group_gpsimd(H1)
         multiply(r[0])
-        read(l[1])
+        read(l[1], "S")
         x_copy(3)
+        read(r[0])
         end(l[1])
         store(2, 2, LEFT)
-        read(r[0])
         x_quantise(2)
-        w_group_gpsimd(H1)
         end(r[0])
         multiply(l[2])
         multiply(r[1])
@@ -423,65 +444,65 @@ def tile_avey_pa_kernel(tc, x, g, W1, b1, out_0, out_1, out_2):
         right_sum(0, 0)
         right_sum(0, 1)
         right_norm(0)
+        x_quantise(3)
+        w_quantise(H0)
+        multiply(l[3])
         end(l[2])
         store(4, 2, LEFT)
-        x_quantise(3)
         read(r[1])
-        multiply(l[3])
-        w_quantise(H0)
-        end(r[1])
-        right_scale(0, nc.vector)
         read(l[3])
         multiply(h[0])
+        read(h[0], "S")
+        end(r[1])
         w_quantise(H1)
-        end(l[3])
-        store(6, 2, LEFT)
+        right_scale(0, nc.vector)
         multiply(t[0])
+        end(l[3])
+        multiply(h[1])
+        store(6, 2, LEFT)
+        read(t[0])
+        end(t[0])
+        end(h[0])
         right_sum(1, 0)
-        read(h[0])
         right_sum(1, 1)
         right_norm(1)
-        read(t[0])
-        multiply(h[1])
-        end(h[0])
-        store(0, 2, H0)
         multiply(r[2])
-        end(t[0])
         read(h[1])
+        store(0, 2, H0)
         multiply(t[1])
         end(h[1])
-        store(2, 2, H0)
-        store(0, 2, H1)
         read(r[2])
-        right_scale(1, nc.vector)
-        multiply(r[3])
+        multiply(h[2])
         end(r[2])
         read(t[1])
         end(t[1])
-        store(2, 2, H1)
-        multiply(h[2])
-        read(r[3])
-        multiply(t[2])
-        end(r[3])
+        store(0, 2, H1)
+        right_scale(1, nc.vector)
+        store(2, 2, H0)
+        multiply(r[3])
         right_sum(2, 0)
         right_sum(2, 1)
         right_norm(2)
         read(h[2])
         multiply(h[3])
         end(h[2])
+        read(r[3])
+        multiply(t[2])
+        end(r[3])
+        read(h[3])
+        multiply(t[3])
+        store(2, 2, H1)
+        right_scale(2, nc.vector)
         store(4, 2, H0)
-        read(t[2])
-        end(t[2])
-        store(4, 2, H1)
         right_sum(3, 0)
         right_sum(3, 1)
         right_norm(3)
-        read(h[3])
-        multiply(t[3])
         end(h[3])
-        right_scale(2, nc.vector)
-        store(6, 2, H0)
+        read(t[2])
+        end(t[2])
+        store(4, 2, H1)
         read(t[3])
         right_scale(3, nc.vector)
         end(t[3])
+        store(6, 2, H0)
         store(6, 2, H1)

@@ -349,11 +349,14 @@ def tile_avey_pa_kernel(tc, x, g, W1, b1, out_0, out_1, out_2):
                     accum_out=norm2[j][:, i : i + 1],
                 )
 
-        def right_norm(j):
-            floor = EPS_NORM * EPS_NORM
-            over = stage.tile([P, 2], F32, name="over")
-            nc.scalar.activation(out=over[:], in_=norm2[j][:], func=ACT.Relu, bias=-floor)
-            nc.scalar.activation(out=inv_norm[j][:], in_=over[:], func=ACT.Abs_reciprocal_sqrt, bias=floor)
+        over = [keep.tile([P, 2], F32, name="over%d" % j) for j in range(PAIRS)]
+        floor = EPS_NORM * EPS_NORM
+
+        def right_norm(j, unit=()):
+            end(unit[:1])
+            nc.scalar.activation(out=over[j][:], in_=norm2[j][:], func=ACT.Relu, bias=-floor)
+            end(unit[1:])
+            nc.scalar.activation(out=inv_norm[j][:], in_=over[j][:], func=ACT.Abs_reciprocal_sqrt, bias=floor)
 
         def right_scale(j, engine):
             unit_rows = keep.tile([P, 2, HALF], F32, name="unit_rows%d" % j)
@@ -409,7 +412,6 @@ def tile_avey_pa_kernel(tc, x, g, W1, b1, out_0, out_1, out_2):
         x_quantise(0)
         w_quantise(LEFT)
         w_group_gpsimd(RIGHT)
-        V(out=token_bias[:], in_=spread_b1[:])
         x_stats(3)
         x_copy(1)
         l = [pair(j, LEFT) for j in range(PAIRS)]
@@ -421,6 +423,7 @@ def tile_avey_pa_kernel(tc, x, g, W1, b1, out_0, out_1, out_2):
         x_turn(2)
         read(l[0], "S")
         x_norm(3)
+        V(out=token_bias[:], in_=spread_b1[:])
         x_quantise(1)
         w_quantise(RIGHT)
         x_copy(2)
@@ -440,14 +443,13 @@ def tile_avey_pa_kernel(tc, x, g, W1, b1, out_0, out_1, out_2):
         end(r[0])
         multiply(l[2])
         multiply(r[1])
+        x_quantise(3)
+        w_quantise(H0)
         read(l[2])
         right_sum(0, 0)
         right_sum(0, 1)
-        right_norm(0)
-        x_quantise(3)
-        w_quantise(H0)
         multiply(l[3])
-        end(l[2])
+        right_norm(0, l[2])
         store(4, 2, LEFT)
         read(r[1])
         read(l[3])
@@ -465,40 +467,38 @@ def tile_avey_pa_kernel(tc, x, g, W1, b1, out_0, out_1, out_2):
         end(h[0])
         right_sum(1, 0)
         right_sum(1, 1)
-        right_norm(1)
         multiply(r[2])
         read(h[1])
         store(0, 2, H0)
         multiply(t[1])
-        end(h[1])
+        right_norm(1, h[1])
         read(r[2])
         multiply(h[2])
         end(r[2])
         read(t[1])
         end(t[1])
         store(0, 2, H1)
-        right_scale(1, nc.vector)
-        store(2, 2, H0)
         multiply(r[3])
         right_sum(2, 0)
         right_sum(2, 1)
-        right_norm(2)
         read(h[2])
+        store(2, 2, H0)
+        right_scale(1, nc.vector)
         multiply(h[3])
-        end(h[2])
+        right_norm(2, h[2])
         read(r[3])
         multiply(t[2])
         end(r[3])
         read(h[3])
         multiply(t[3])
         store(2, 2, H1)
-        right_scale(2, nc.vector)
-        store(4, 2, H0)
         right_sum(3, 0)
         right_sum(3, 1)
         right_norm(3)
         end(h[3])
+        store(4, 2, H0)
         read(t[2])
+        right_scale(2, nc.vector)
         end(t[2])
         store(4, 2, H1)
         read(t[3])

@@ -78,6 +78,8 @@ def tile_avey_pa_kernel(tc, x, g, W1, b1, out_0, out_1, out_2):
 
         consts = keep.tile([P, BANK], BF16)
         nc.vector.memset(consts[:], 0.0)
+        zeros = keep.tile([P, BANK], BF16)
+        nc.vector.memset(zeros[:], 0.0)
         warm = keep.tile([P, 1], F32)
         nc.vector.memset(warm[:], 1.0)
         nc.scalar.activation(out=warm[:], in_=warm[:], func=ACT.Abs_reciprocal_sqrt)
@@ -117,6 +119,12 @@ def tile_avey_pa_kernel(tc, x, g, W1, b1, out_0, out_1, out_2):
             for c in range(GROUPS):
                 nc.tensor.transpose(turned[:, c, :], consts[:, c * P : (c + 1) * P], ident[:])
             return turned
+
+        idle = psum_acc.tile([P, BANK], F32, tag="acc", name="idle")
+
+        def keep_clock(passes):
+            for i in range(passes):
+                nc.tensor.matmul(out=idle[:], lhsT=ident[:], rhs=zeros[:], start=True, stop=True)
 
         ready = set()
 
@@ -392,6 +400,7 @@ def tile_avey_pa_kernel(tc, x, g, W1, b1, out_0, out_1, out_2):
             for share in shares:
                 finish(share)
 
+        keep_clock(3)
         x_square(0)
         x_rstd(0, slice(0, 1))
         x_square(1, "V")
@@ -404,6 +413,7 @@ def tile_avey_pa_kernel(tc, x, g, W1, b1, out_0, out_1, out_2):
         x_norm(0)
         V(out=bias[:], in_=turned_bias[:, :, 0:BANKS])
         x_turn(0)
+        keep_clock(2)
         x_copy(0)
         w_group(LEFT, V)
         x_stats(2)
@@ -421,13 +431,16 @@ def tile_avey_pa_kernel(tc, x, g, W1, b1, out_0, out_1, out_2):
         multiply(l[0])
         x_norm(2)
         x_turn(2)
+        keep_clock(1)
         read(l[0], "S")
         x_norm(3)
         V(out=token_bias[:], in_=spread_b1[:])
         x_quantise(1)
         w_quantise(RIGHT)
         x_copy(2)
-        end(l[0])
+        end(l[0][:1])
+        keep_clock(1)
+        end(l[0][1:])
         store(0, 2, LEFT)
         multiply(l[1])
         x_turn(3)

@@ -122,9 +122,11 @@ def tile_avey_pa_kernel(tc, x, g, W1, b1, out_0, out_1, out_2):
 
         idle = psum_acc.tile([P, BANK], F32, tag="acc", name="idle")
 
-        def keep_clock(passes):
+        def keep_clock(passes, operand=zeros[:], idle=idle):
             for i in range(passes):
-                nc.tensor.matmul(out=idle[:], lhsT=ident[:], rhs=zeros[:], start=True, stop=True)
+                nc.tensor.matmul(
+                    out=idle[:, 0 : operand.shape[1]], lhsT=ident[:], rhs=operand, start=True, stop=True
+                )
 
         ready = set()
 
@@ -415,10 +417,12 @@ def tile_avey_pa_kernel(tc, x, g, W1, b1, out_0, out_1, out_2):
         x_turn(0)
         keep_clock(2)
         x_copy(0)
+        keep_clock(2, x_grouped[0][:].rearrange("p h r t -> p (h r t)")[:, 0:BANK])
         w_group(LEFT, V)
         x_stats(2)
         x_norm(1)
         x_turn(1)
+        keep_clock(1, zeros[:, 0 : 2 * P])
         x_quantise(0)
         w_quantise(LEFT)
         w_group_gpsimd(RIGHT)
@@ -451,6 +455,8 @@ def tile_avey_pa_kernel(tc, x, g, W1, b1, out_0, out_1, out_2):
         x_copy(3)
         read(r[0])
         end(l[1])
+        idle_late = psum_acc.tile([P, BANK], F32, tag="acc", name="idle_late")
+        keep_clock(1, idle=idle_late)
         store(2, 2, LEFT)
         x_quantise(2)
         end(r[0])

@@ -90,10 +90,10 @@ def tile_avey_pa_kernel(tc, x, g, W1, b1, out_0, out_1, out_2):
         load_x(1)
         load_w(LEFT)
         load_x(2)
-        load_w(RIGHT)
-        load_x(3)
         load_w(H0)
+        load_x(3)
         load_w(H1)
+        load_w(RIGHT)
 
         ident = keep.tile([P, P], BF16)
         masks.make_identity(nc, ident[:])
@@ -333,11 +333,11 @@ def tile_avey_pa_kernel(tc, x, g, W1, b1, out_0, out_1, out_2):
 
         def store(first, tiles, b):
             rows, left = outputs[b]
-            for i in range(0, tiles, 2):
-                nc.sync.dma_start(
-                    out=rows[:, first + i : first + i + 2, left : left + BANK],
-                    in_=enriched[first, b][:, i : i + 2, :],
-                )
+            pair_tile = enriched[first - first % 2, b]
+            nc.sync.dma_start(
+                out=rows[:, first : first + tiles, left : left + BANK],
+                in_=pair_tile[:, first % 2 : first % 2 + tiles, :],
+            )
 
 
         norm2 = [keep.tile([P, 2], F32, name="norm2_%d" % j) for j in range(PAIRS)]
@@ -425,7 +425,7 @@ def tile_avey_pa_kernel(tc, x, g, W1, b1, out_0, out_1, out_2):
         keep_clock(1, zeros[:, 0 : 2 * P])
         x_quantise(0)
         w_quantise(LEFT)
-        w_group_gpsimd(RIGHT)
+        w_group_gpsimd(H0)
         x_stats(3)
         x_copy(1)
         l = [pair(j, LEFT) for j in range(PAIRS)]
@@ -440,88 +440,90 @@ def tile_avey_pa_kernel(tc, x, g, W1, b1, out_0, out_1, out_2):
         x_norm(3)
         V(out=token_bias[:], in_=spread_b1[:])
         x_quantise(1)
-        w_quantise(RIGHT)
+        w_quantise(H0)
         x_copy(2)
         end(l[0][:1])
         keep_clock(1)
         end(l[0][1:])
         store(0, 2, LEFT)
         multiply(l[1])
-        x_turn(3)
-        w_group(H0, V)
-        w_group_gpsimd(H1)
-        multiply(r[0])
-        read(l[1], "S")
-        x_copy(3)
-        read(r[0])
-        end(l[1])
-        idle_late = psum_acc.tile([P, BANK], F32, tag="acc", name="idle_late")
-        keep_clock(1, idle=idle_late)
-        store(2, 2, LEFT)
-        x_quantise(2)
-        end(r[0])
-        multiply(l[2])
-        multiply(r[1])
-        x_quantise(3)
-        w_quantise(H0)
-        read(l[2])
-        right_sum(0, 0)
-        right_sum(0, 1)
-        multiply(l[3])
-        right_norm(0, l[2])
-        store(4, 2, LEFT)
-        read(r[1])
-        read(l[3])
         multiply(h[0])
-        read(h[0], "S")
-        end(r[1])
-        w_quantise(H1)
-        right_scale(0, nc.vector)
-        multiply(t[0])
-        end(l[3])
+        x_quantise(2)
+        w_group_gpsimd(H1)
+        read(l[1])
+        x_turn(3)
+        read(h[0][:1])
+        read(h[0][1:], "S")
+        x_copy(3)
+        idle_late = psum_acc.tile([P, BANK], F32, tag="acc", name="idle_late")
+        multiply(l[2][:1])
+        end(l[1][:1])
+        multiply(l[2][1:])
+        end(l[1][1:])
+        store(2, 2, LEFT)
+        read(l[2])
+        end(h[0])
+        store(0, 2, H0)
         multiply(h[1])
-        store(6, 2, LEFT)
+        x_quantise(3)
+        w_quantise(H1)
+        w_group_gpsimd(RIGHT)
+        multiply(l[3])
+        end(l[2])
+        store(4, 2, LEFT)
+        read(h[1])
+        read(l[3])
+        multiply(t[0])
+        end(h[1])
+        store(2, 2, H0)
+        multiply(h[2])
+        read(h[2], "S")
         read(t[0])
         end(t[0])
-        end(h[0])
-        right_sum(1, 0)
-        right_sum(1, 1)
-        multiply(r[2])
-        read(h[1])
-        store(0, 2, H0)
+        end(l[3])
+        store(6, 2, LEFT)
+        w_quantise(RIGHT)
+        multiply(r[0])
+        multiply(h[3])
+        end(h[2])
+        store(4, 2, H0)
+        read(r[0])
+        multiply(r[1])
+        end(r[0])
+        read(h[3])
         multiply(t[1])
-        right_norm(1, h[1])
-        read(r[2])
-        multiply(h[2])
-        end(r[2])
+        end(h[3])
+        store(0, 2, H1)
+        store(6, 2, H0)
+        right_sum(0, 0)
+        right_sum(0, 1)
+        read(r[1])
+        multiply(r[2])
+        right_norm(0, r[1])
         read(t[1])
         end(t[1])
-        store(0, 2, H1)
         multiply(r[3])
+        read(r[2])
+        multiply(t[2])
+        right_sum(1, 0)
+        right_sum(1, 1)
+        right_norm(1, r[2])
+        read(r[3])
+        multiply(t[3])
         right_sum(2, 0)
         right_sum(2, 1)
-        read(h[2])
-        store(2, 2, H0)
-        right_scale(1, nc.vector)
-        multiply(h[3])
-        right_norm(2, h[2])
-        read(r[3])
-        multiply(t[2])
-        end(r[3])
-        read(h[3])
-        multiply(t[3])
-        store(2, 2, H1)
-        right_sum(3, 0)
-        right_sum(3, 1)
-        right_norm(3)
-        end(h[3])
-        store(4, 2, H0)
         read(t[2])
-        right_scale(2, nc.vector)
+        store(2, 2, H1)
+        right_scale(0, nc.vector)
+        right_norm(2, r[3])
         end(t[2])
         store(4, 2, H1)
+        right_sum(3, 0)
         read(t[3])
-        right_scale(3, nc.vector)
+        right_scale(1, nc.vector)
         end(t[3])
-        store(6, 2, H0)
         store(6, 2, H1)
+        right_sum(3, 1, "V")
+        right_norm(3)
+        right_scale(2, nc.vector)
+        right_scale(3, nc.vector)

@@ -362,11 +362,17 @@ def tile_avey_pa_kernel(tc, x, g, W1, b1, out_0, out_1, out_2):
         over = [keep.tile([P, 2], F32, name="over%d" % j) for j in range(PAIRS)]
         floor = EPS_NORM * EPS_NORM
 
+        def right_floor(j):
+            nc.scalar.activation(out=over[j][:], in_=norm2[j][:], func=ACT.Relu, bias=-floor)
+
+        def right_invert(j):
+            nc.scalar.activation(out=inv_norm[j][:], in_=over[j][:], func=ACT.Abs_reciprocal_sqrt, bias=floor)
+
         def right_norm(j, unit=()):
             end(unit[:1])
-            nc.scalar.activation(out=over[j][:], in_=norm2[j][:], func=ACT.Relu, bias=-floor)
+            right_floor(j)
             end(unit[1:])
-            nc.scalar.activation(out=inv_norm[j][:], in_=over[j][:], func=ACT.Abs_reciprocal_sqrt, bias=floor)
+            right_invert(j)
 
         def right_scale(j, engine):
             unit_rows = keep.tile([P, 2, HALF], F32, name="unit_rows%d" % j)
@@ -455,7 +461,6 @@ def tile_avey_pa_kernel(tc, x, g, W1, b1, out_0, out_1, out_2):
         read(h[0][:1])
         read(h[0][1:], "S")
         x_copy(3)
-        idle_late = psum_acc.tile([P, BANK], F32, tag="acc", name="idle_late")
         multiply(l[2][:1])
         end(l[1][:1])
         multiply(l[2][1:])
@@ -477,34 +482,36 @@ def tile_avey_pa_kernel(tc, x, g, W1, b1, out_0, out_1, out_2):
         end(h[1])
         store(2, 2, H0)
         multiply(h[2])
-        read(h[2], "S")
         read(t[0])
         end(t[0])
         end(l[3])
         store(6, 2, LEFT)
         w_quantise(RIGHT)
+        read(h[2])
         multiply(r[0])
         multiply(h[3])
+        read(h[3][1:], "S")
         end(h[2])
         store(4, 2, H0)
         read(r[0])
-        multiply(r[1])
-        end(r[0])
-        read(h[3])
         multiply(t[1])
+        end(r[0])
+        read(h[3][:1])
+        multiply(r[1])
+        read(t[1])
+        end(t[1])
         end(h[3])
         store(0, 2, H1)
         store(6, 2, H0)
+        multiply(r[2])
         right_sum(0, 0)
         right_sum(0, 1)
         read(r[1])
-        multiply(r[2])
-        right_norm(0, r[1])
-        read(t[1])
-        end(t[1])
         multiply(r[3])
+        right_norm(0, r[1])
         read(r[2])
         multiply(t[2])
+        store(2, 2, H1)
         right_sum(1, 0)
         right_sum(1, 1)
         right_norm(1, r[2])
@@ -513,7 +520,6 @@ def tile_avey_pa_kernel(tc, x, g, W1, b1, out_0, out_1, out_2):
         right_sum(2, 0)
         right_sum(2, 1)
         read(t[2])
-        store(2, 2, H1)
         right_scale(0, nc.vector)
         right_norm(2, r[3])
         end(t[2])

@@ -13,22 +13,25 @@ ALU = mybir.AluOpType
 
 P = 128
 PACK = 4
+MX_ALIGN = 64
 TOKENS = 1024
 D = 512
 HEAD = 1024
 HALF = 512
 E = HEAD + HALF + HALF
 BANK = 512
-TOK_TILES = TOKENS // P
-GPSIMD_TOKENS = (0, 1, 2, 3)
-FLT_MAX = 3.4028234663852886e38
-PAIRS = TOK_TILES // 2
-QUAD = 4
-GROUPS = BANK // P
 BANKS = E // BANK
+GROUPS = BANK // P
+TOK_TILES = TOKENS // P
+PAIR = 2
+PAIRS = TOK_TILES // PAIR
+WIDTH = BANK // (PAIR * P)
+GPSIMD_TOKENS = TOK_TILES // 2
 GAIN_ROW = BANKS
+FLT_MAX = 3.4028234663852886e38
 EPS_RMS = 1e-6
 EPS_NORM = 1e-12
+EPS_NORM_SQUARED = EPS_NORM * EPS_NORM
 
 FLOPS = 2 * TOKENS * D * E
 
@@ -36,18 +39,21 @@ FLOPS = 2 * TOKENS * D * E
 def tile_avey_pa_kernel(tc, x, g, W1, b1, out_0, out_1, out_2):
     nc = tc.nc
 
-    x_rows = x.flatten_outer_dims().rearrange("(p i) k -> p i k", i=TOK_TILES)
-    head_rows = out_0.flatten_outer_dims().rearrange("(p i) f -> p i f", i=TOK_TILES)
-    left_rows = out_1.flatten_outer_dims().rearrange("(p i) f -> p i f", i=TOK_TILES)
-    right_rows = out_2.flatten_outer_dims().rearrange("(p i) f -> p i f", i=TOK_TILES)
+    def token_rows(tensor):
+        return tensor.flatten_outer_dims().rearrange("(p i) k -> p i k", i=TOK_TILES)
+
+    x_rows = token_rows(x)
     w_rows = W1.rearrange("(p t) f -> p t f", t=PACK)
 
     H0, H1, LEFT, RIGHT = range(BANKS)
     UNIT = BANKS
-    outputs = {H0: (head_rows, 0), H1: (head_rows, BANK), LEFT: (left_rows, 0), UNIT: (right_rows, 0)}
-
-    def cols(b):
-        return slice(b * BANK, (b + 1) * BANK)
+    head_rows = token_rows(out_0)
+    outputs = {
+        H0: head_rows[:, :, 0:BANK],
+        H1: head_rows[:, :, BANK:HEAD],
+        LEFT: token_rows(out_1),
+        UNIT: token_rows(out_2),
+    }
 
     with ExitStack() as ctx:
         keep = ctx.enter_context(tc.tile_pool(name="keep", bufs=1))
@@ -59,22 +65,16 @@ def tile_avey_pa_kernel(tc, x, g, W1, b1, out_0, out_1, out_2):
         psum_acc = ctx.enter_context(tc.psum_pool(name="psum_acc", bufs=4))
         ctx.enter_context(tc.manual_schedule())
 
-        x_first = [keep.tile([P, 1, D], BF16, name="x_first%d" % i) for i in range(2)]
-        x_pairs = [keep.tile([P, 2, D], BF16, name="x_pair%d" % j) for j in range(1, PAIRS)]
-        x_sb = [x_first[0][:, 0, :], x_first[1][:, 0, :]]
-        for pair_tile in x_pairs:
-            x_sb += [pair_tile[:, 0, :], pair_tile[:, 1, :]]
+        x_first = [keep.tile([P, 1, D], BF16, name="x_first%d" % i) for i in range(PAIR)]
+        x_pairs = [keep.tile([P, PAIR, D], BF16, name="x_pair%d" % j) for j in range(1, PAIRS)]
+        x_sb = [tile[:, 0, :] for tile in x_first] + [tile[:, i, :] for tile in x_pairs for i in range(PAIR)]
         w_raw = [keep.tile([P, PACK, BANK], BF16, name="w_raw%d" % b) for b in range(BANKS)]
 
         def load_x(j):
-            if j == 0:
-                for i in range(2):
-                    nc.sync.dma_start(out=x_first[i][:], in_=x_rows[:, i : i + 1, :])
-                return
-            nc.sync.dma_start(out=x_pairs[j - 1][:], in_=x_rows[:, 2 * j : 2 * j + 2, :])
+            nc.sync.dma_start(out=x_pairs[j - 1][:], in_=x_rows[:, PAIR * j : PAIR * (j + 1), :])
 
         def load_w(b):
-            nc.sync.dma_start(out=w_raw[b][:], in_=w_rows[:, :, cols(b)])
+            nc.sync.dma_start(out=w_raw[b][:], in_=w_rows[:, :, b * BANK : (b + 1) * BANK])
 
         consts = keep.tile([P, BANK], BF16)
         nc.vector.memset(consts[:], 0.0)
@@ -84,7 +84,8 @@ def tile_avey_pa_kernel(tc, x, g, W1, b1, out_0, out_1, out_2):
         nc.vector.memset(warm[:], 1.0)
         nc.scalar.activation(out=warm[:], in_=warm[:], func=ACT.Abs_reciprocal_sqrt)
 
-        load_x(0)
+        for i in range(PAIR):
+            nc.sync.dma_start(out=x_first[i][:], in_=x_rows[:, i : i + 1, :])
         nc.sync.dma_start(out=consts[GAIN_ROW : GAIN_ROW + 1, :], in_=g.unsqueeze(0))
         nc.sync.dma_start(out=consts[0:BANKS, :], in_=b1.rearrange("(r c) -> r c", c=BANK))
         load_x(1)
@@ -102,7 +103,6 @@ def tile_avey_pa_kernel(tc, x, g, W1, b1, out_0, out_1, out_2):
 
         gain = psum_gain.tile([P, D], BF16, tag="gain")
         bias = keep.tile([P, GROUPS, BANKS], F32)
-
         token_bias = keep.tile([P, BANK], BF16)
 
         def spread(row, acc):
@@ -122,62 +122,57 @@ def tile_avey_pa_kernel(tc, x, g, W1, b1, out_0, out_1, out_2):
 
         idle = psum_acc.tile([P, BANK], F32, tag="acc", name="idle")
 
-        def keep_clock(passes, operand=zeros[:], idle=idle):
-            for i in range(passes):
-                nc.tensor.matmul(
-                    out=idle[:, 0 : operand.shape[1]], lhsT=ident[:], rhs=operand, start=True, stop=True
-                )
+        def keep_clock(operand):
+            nc.tensor.matmul(out=idle[:, 0 : operand.shape[1]], lhsT=ident[:], rhs=operand, start=True, stop=True)
 
-        ready = set()
+        def mx_tile(shape, dtype, name):
+            return keep.tile(shape, dtype, align_bytes=MX_ALIGN, name=name)
 
-        x_codes = [keep.tile([P, BANK], U32, align_bytes=64, name="x_codes%d" % q) for q in range(TOK_TILES // QUAD)]
-        x_scales = [keep.tile([P, BANK], U8, align_bytes=64, name="x_scales%d" % q) for q in range(TOK_TILES // QUAD)]
-        w_codes = [keep.tile([P, BANK], U32, align_bytes=64, name="w_codes%d" % b) for b in range(BANKS)]
-        w_scales = [keep.tile([P, BANK], U8, align_bytes=64, name="w_scales%d" % b) for b in range(BANKS)]
-        x_grouped = [keep.tile([P, 2, P, PACK], BF16, align_bytes=64, name="x_grouped%d" % j) for j in range(PAIRS)]
-        w_grouped = [keep.tile([P, BANK, PACK], BF16, align_bytes=64, name="w_grouped%d" % b) for b in range(BANKS)]
-        sumsq = [keep.tile([P, 2], F32, name="sumsq%d" % j) for j in range(PAIRS)]
-        rstd = [keep.tile([P, 2], F32, name="rstd%d" % j) for j in range(PAIRS)]
+        x_grouped = [mx_tile([P, PAIR * P * PACK], BF16, "x_grouped%d" % j) for j in range(PAIRS)]
+        x_codes = [mx_tile([P, PAIR * P], U32, "x_codes%d" % j) for j in range(PAIRS)]
+        x_scales = [mx_tile([P, PAIR * P], U8, "x_scales%d" % j) for j in range(PAIRS)]
+        w_grouped = [mx_tile([P, BANK, PACK], BF16, "w_grouped%d" % b) for b in range(BANKS)]
+        w_codes = [mx_tile([P, BANK], U32, "w_codes%d" % b) for b in range(BANKS)]
+        w_scales = [mx_tile([P, BANK], U8, "w_scales%d" % b) for b in range(BANKS)]
+        square_sums = [keep.tile([P, PAIR], F32, name="square_sums%d" % j) for j in range(PAIRS)]
+        rstd = [keep.tile([P, PAIR], F32, name="rstd%d" % j) for j in range(PAIRS)]
 
-        def x_square(i, engine="S"):
-            squares = stage.tile([P, D], BF16, name="squares" + engine)
-            total = sumsq[i // 2][:, i % 2 : i % 2 + 1]
+        def sum_squares(engine, rows, total):
+            unread = stage.tile([P, BANK], BF16, name="unread" + engine)
             if engine == "S":
-                nc.scalar.activation(out=squares[:], in_=x_sb[i], func=ACT.Square, accum_out=total)
+                nc.scalar.activation(out=unread[:], in_=rows, func=ACT.Square, accum_out=total)
             else:
                 nc.vector.scalar_tensor_tensor(
-                    out=squares[:],
-                    in0=x_sb[i],
-                    scalar=1.0,
-                    in1=x_sb[i],
-                    op0=ALU.mult,
-                    op1=ALU.mult,
-                    accum_out=total,
+                    out=unread[:], in0=rows, scalar=1.0, in1=rows, op0=ALU.mult, op1=ALU.mult, accum_out=total
                 )
 
-        def x_rstd(j, here=slice(0, 2)):
+        def x_sum(i, engine="S"):
+            j, h = divmod(i, PAIR)
+            sum_squares(engine, x_sb[i], square_sums[j][:, h : h + 1])
+
+        def x_rstd(j, here=slice(0, PAIR)):
             nc.scalar.activation(
                 out=rstd[j][:, here],
-                in_=sumsq[j][:, here],
+                in_=square_sums[j][:, here],
                 func=ACT.Abs_reciprocal_sqrt,
                 bias=EPS_RMS,
                 scale=1.0 / D,
             )
 
         def x_stats(j):
-            x_square(2 * j)
-            x_square(2 * j + 1)
+            for h in range(PAIR):
+                x_sum(PAIR * j + h)
             x_rstd(j)
 
-        xns = {}
-        turneds = {}
+        normed = {}
+        turned_x = {}
 
         def x_norm(j):
-            xns[j] = xn = stage.tile([P, 2, D], BF16, name="xn")
-            for h in range(2):
+            normed[j] = xn = stage.tile([P, PAIR, D], BF16, name="xn")
+            for h in range(PAIR):
                 nc.vector.scalar_tensor_tensor(
                     out=xn[:, h, :],
-                    in0=x_sb[2 * j + h],
+                    in0=x_sb[PAIR * j + h],
                     scalar=rstd[j][:, h : h + 1],
                     in1=gain[:],
                     op0=ALU.mult,
@@ -185,43 +180,32 @@ def tile_avey_pa_kernel(tc, x, g, W1, b1, out_0, out_1, out_2):
                 )
 
         def x_turn(j):
-            words = xns[j][:].bitcast(F32)
-            turned = psum_turn.tile([P, 2, 2, P], F32, tag="turn", name="turn")
-            for h in range(2):
-                for u in range(2):
-                    nc.tensor.transpose(turned[:, h, u, :], words[:, h, u::2], ident_f32[:])
-            turneds[j] = turned
+            words = normed[j][:].bitcast(F32)
+            turned_x[j] = turned = psum_turn.tile([P, PAIR, PACK // 2, P], F32, tag="turn", name="turn")
+            for h in range(PAIR):
+                for u in range(PACK // 2):
+                    nc.tensor.transpose(turned[:, h, u, :], words[:, h, u :: PACK // 2], ident_f32[:])
 
         def x_copy(j):
             nc.scalar.copy(
-                out=x_grouped[j][:].rearrange("p h r t -> p (h r t)").bitcast(F32),
-                in_=turneds[j][:].rearrange("p h u r -> p h r u"),
+                out=x_grouped[j][:].bitcast(F32),
+                in_=turned_x[j][:].rearrange("p h u r -> p h r u"),
             )
-
-        def token_columns(first, tiles):
-            q, t = divmod(first, QUAD)
-            return q, slice(t * P, (t + tiles) * P)
 
         def x_quantise(j):
-            q, toks = token_columns(2 * j, 2)
-            nc.vector.quantize_mx(
-                out=x_codes[q][:, toks].bitcast(FP8X4),
-                scales=x_scales[q][:, toks],
-                in_=x_grouped[j][:].rearrange("p h r t -> p (h r t)"),
-            )
-            ready.add(("x", j))
+            nc.vector.quantize_mx(out=x_codes[j][:].bitcast(FP8X4), scales=x_scales[j][:], in_=x_grouped[j][:])
 
-        def w_group(b, copy, first=0, last=BANK):
-            copy(
-                out=w_grouped[b][:, first:last, :].rearrange("p (c i) t -> p c t i", i=4),
-                in_=w_raw[b][:, :, first:last].rearrange("p t (c i) -> p c t i", i=4),
+        def w_group(b):
+            nc.vector.tensor_copy(
+                out=w_grouped[b][:].rearrange("p (c i) t -> p c t i", i=PACK),
+                in_=w_raw[b][:].rearrange("p t (c i) -> p c t i", i=PACK),
             )
 
-        def w_group_gpsimd(b, wait=True):
+        def w_group_gpsimd(b):
             go = keep.tile([P, 1], F32, name="go%d" % b)
             nc.vector.memset(go[:], 1.0)
             for half in range(2):
-                here = slice(half * 2 * P, (half + 1) * 2 * P)
+                here = slice(half * BANK // 2, (half + 1) * BANK // 2)
                 nc.gpsimd.tensor_scalar(
                     out=w_grouped[b][:, here, :],
                     in0=w_raw[b][:, :, here].rearrange("p t f -> p f t"),
@@ -237,164 +221,139 @@ def tile_avey_pa_kernel(tc, x, g, W1, b1, out_0, out_1, out_2):
                 scales=w_scales[b][:],
                 in_=w_grouped[b][:].rearrange("p f t -> p (f t)"),
             )
-            ready.add(("w", b))
 
         enriched = {}
-        accs = {}
-        mids = {}
+        products = {}
+        reads = {}
         turns = []
 
         def matmul(share):
-            accs[share] = acc = psum_acc.tile([P, BANK], F32, tag="acc", name="acc")
+            products[share] = acc = psum_acc.tile([P, BANK], F32, tag="acc", name="acc")
             if len(share) == 1:
-                q, toks = token_columns(share[0], 1)
+                j, h = divmod(share[0], PAIR)
+                toks = slice(h * P, (h + 1) * P)
                 nc.tensor.matmul_mx(
                     out=acc[:],
-                    lhsT=x_codes[q][:, toks].bitcast(FP8X4),
-                    lhsT_scale=x_scales[q][:, toks],
+                    lhsT=x_codes[j][:, toks].bitcast(FP8X4),
+                    lhsT_scale=x_scales[j][:, toks],
                     rhs=w_codes[H1][:].bitcast(FP8X4),
                     rhs_scale=w_scales[H1][:],
                     start=True,
                     stop=True,
                 )
                 return
-            first, tiles, b, c = share
-            q, toks = token_columns(first, tiles)
-            for n in range(QUAD // tiles):
+            j, b, c = share
+            for n in range(WIDTH):
                 feats = slice((c + n) * P, (c + n + 1) * P)
                 nc.tensor.matmul_mx(
-                    out=acc[:, n * tiles * P : (n + 1) * tiles * P],
+                    out=acc[:, n * PAIR * P : (n + 1) * PAIR * P],
                     lhsT=w_codes[b][:, feats].bitcast(FP8X4),
                     lhsT_scale=w_scales[b][:, feats],
-                    rhs=x_codes[q][:, toks].bitcast(FP8X4),
-                    rhs_scale=x_scales[q][:, toks],
+                    rhs=x_codes[j][:].bitcast(FP8X4),
+                    rhs_scale=x_scales[j][:],
                     start=True,
                     stop=True,
                 )
 
         def drain(share, engine):
-            acc = accs[share]
+            acc = products[share]
             if len(share) == 1:
-                mids[share] = mid = tokens.tile([P, BANK], F32, name="mid")
+                reads[share] = mid = tokens.tile([P, BANK], F32, name="mid")
                 nc.vector.tensor_tensor(out=mid[:], in0=acc[:], in1=token_bias[:], op=ALU.add)
                 return
-            first, tiles, b, c = share
-            mids[share] = mid = flip.tile([P, BANK], F32, name="flat")
-            for n in range(QUAD // tiles):
-                part = slice(n * tiles * P, (n + 1) * tiles * P)
+            j, b, c = share
+            reads[share] = mid = flip.tile([P, BANK], F32, name="mid_flip")
+            for n in range(WIDTH):
+                part = slice(n * PAIR * P, (n + 1) * PAIR * P)
+                b1_column = bias[:, c + n, b : b + 1]
                 if engine == "S":
-                    nc.scalar.activation(
-                        out=mid[:, part], in_=acc[:, part], func=ACT.Relu, bias=bias[:, c + n, b : b + 1]
-                    )
+                    nc.scalar.activation(out=mid[:, part], in_=acc[:, part], func=ACT.Relu, bias=b1_column)
                 else:
                     nc.vector.tensor_scalar(
                         out=mid[:, part],
                         in0=acc[:, part],
-                        scalar1=bias[:, c + n, b : b + 1],
+                        scalar1=b1_column,
                         scalar2=0.0,
                         op0=ALU.add,
                         op1=ALU.max,
                     )
 
-        def finish(share):
-            mid = mids[share]
-            if len(share) == 1:
-                i = share[0]
-                if i % 2 == 0:
-                    enriched[i, H1] = keep.tile([P, 2, BANK], F32, name="enriched_h1_%d" % i)
-                result = enriched[i - i % 2, H1]
-                if i not in GPSIMD_TOKENS:
-                    nc.vector.scalar_tensor_tensor(
-                        out=result[:, i % 2, :], in0=mid[:], scalar=0.0, in1=mid[:], op0=ALU.max, op1=ALU.mult
-                    )
-                    return
-                above = tokens.tile([P, BANK], F32, name="above")
-                nc.gpsimd.tensor_scalar(
-                    out=above[:], in0=mid[:], scalar1=FLT_MAX, scalar2=0.0, op0=ALU.min, op1=ALU.max
+        def finish_tokens(i):
+            mid = reads[(i,)]
+            j, h = divmod(i, PAIR)
+            if h == 0:
+                enriched[j, H1] = keep.tile([P, PAIR, BANK], F32, name="enriched_h1_%d" % j)
+            result = enriched[j, H1][:, h, :]
+            if i >= GPSIMD_TOKENS:
+                nc.vector.scalar_tensor_tensor(
+                    out=result, in0=mid[:], scalar=0.0, in1=mid[:], op0=ALU.max, op1=ALU.mult
                 )
-                nc.gpsimd.tensor_tensor(out=result[:, i % 2, :], in0=above[:], in1=above[:], op=ALU.mult)
                 return
-            first, tiles, b, c = share
+            above = tokens.tile([P, BANK], F32, name="above")
+            nc.gpsimd.tensor_scalar(
+                out=above[:], in0=mid[:], scalar1=FLT_MAX, scalar2=0.0, op0=ALU.min, op1=ALU.max
+            )
+            nc.gpsimd.tensor_tensor(out=result, in0=above[:], in1=above[:], op=ALU.mult)
+
+        def finish(share):
+            if len(share) == 1:
+                finish_tokens(share[0])
+                return
+            mid = reads[share]
+            j, b, c = share
             if c == 0:
-                enriched[first, b] = keep.tile([P, tiles, BANK], F32, name="enriched%d%d" % (first, b))
-            width = QUAD // tiles
+                enriched[j, b] = keep.tile([P, PAIR, BANK], F32, name="enriched%d_%d" % (b, j))
             pool, tag = (psum_gain, "gain") if len(turns) % 4 == 3 else (psum_turn, "turn")
             turns.append(share)
-            turned = pool.tile([P, tiles, width, P], F32, tag=tag, name="turn")
-            for n in range(width):
-                for i in range(tiles):
-                    tok = slice((n * tiles + i) * P, (n * tiles + i + 1) * P)
-                    nc.tensor.transpose(turned[:, i, n, :], mid[:, tok], ident_f32[:])
+            turned = pool.tile([P, PAIR, WIDTH, P], F32, tag=tag, name="turn")
+            for n in range(WIDTH):
+                for h in range(PAIR):
+                    toks = slice((n * PAIR + h) * P, (n * PAIR + h + 1) * P)
+                    nc.tensor.transpose(turned[:, h, n, :], mid[:, toks], ident_f32[:])
             nc.scalar.activation(
-                out=enriched[first, b][:, :, c * P : (c + width) * P],
-                in_=turned[:].rearrange("p i n r -> p i (n r)"),
+                out=enriched[j, b][:, :, c * P : (c + WIDTH) * P],
+                in_=turned[:].rearrange("p h n r -> p h (n r)"),
                 func=ACT.Square,
             )
 
-        def store(first, tiles, b):
-            rows, left = outputs[b]
-            pair_tile = enriched[first - first % 2, b]
-            nc.sync.dma_start(
-                out=rows[:, first : first + tiles, left : left + BANK],
-                in_=pair_tile[:, first % 2 : first % 2 + tiles, :],
-            )
+        def store(j, b):
+            nc.sync.dma_start(out=outputs[b][:, PAIR * j : PAIR * (j + 1), :], in_=enriched[j, b][:])
 
+        norm2 = [keep.tile([P, PAIR], F32, name="norm2_%d" % j) for j in range(PAIRS)]
+        over = [keep.tile([P, PAIR], F32, name="over%d" % j) for j in range(PAIRS)]
+        inv_norm = [keep.tile([P, PAIR], F32, name="inv_norm%d" % j) for j in range(PAIRS)]
 
-        norm2 = [keep.tile([P, 2], F32, name="norm2_%d" % j) for j in range(PAIRS)]
-        inv_norm = [keep.tile([P, 2], F32, name="inv_norm%d" % j) for j in range(PAIRS)]
-
-        def right_sum(j, i, engine="S"):
-            rows = enriched[2 * j, RIGHT][:, i, :]
-            fourth = stage.tile([P, HALF], BF16, name="fourth" + engine)
-            if engine == "S":
-                nc.scalar.activation(out=fourth[:], in_=rows, func=ACT.Square, accum_out=norm2[j][:, i : i + 1])
-            else:
-                nc.vector.scalar_tensor_tensor(
-                    out=fourth[:],
-                    in0=rows,
-                    scalar=1.0,
-                    in1=rows,
-                    op0=ALU.mult,
-                    op1=ALU.mult,
-                    accum_out=norm2[j][:, i : i + 1],
-                )
-
-        over = [keep.tile([P, 2], F32, name="over%d" % j) for j in range(PAIRS)]
-        floor = EPS_NORM * EPS_NORM
+        def right_sum(j, h, engine="S"):
+            sum_squares(engine, enriched[j, RIGHT][:, h, :], norm2[j][:, h : h + 1])
 
         def right_floor(j):
-            nc.scalar.activation(out=over[j][:], in_=norm2[j][:], func=ACT.Relu, bias=-floor)
+            nc.scalar.activation(out=over[j][:], in_=norm2[j][:], func=ACT.Relu, bias=-EPS_NORM_SQUARED)
 
         def right_invert(j):
-            nc.scalar.activation(out=inv_norm[j][:], in_=over[j][:], func=ACT.Abs_reciprocal_sqrt, bias=floor)
+            nc.scalar.activation(
+                out=inv_norm[j][:], in_=over[j][:], func=ACT.Abs_reciprocal_sqrt, bias=EPS_NORM_SQUARED
+            )
 
-        def right_norm(j, unit=()):
-            end(unit[:1])
-            right_floor(j)
-            end(unit[1:])
-            right_invert(j)
-
-        def right_scale(j, engine):
-            unit_rows = keep.tile([P, 2, HALF], F32, name="unit_rows%d" % j)
-            for i in range(2):
-                engine.tensor_scalar(
-                    out=unit_rows[:, i, :],
-                    in0=enriched[2 * j, RIGHT][:, i, :],
-                    scalar1=inv_norm[j][:, i : i + 1],
+        def right_store(j):
+            enriched[j, UNIT] = unit_rows = keep.tile([P, PAIR, HALF], F32, name="unit_rows%d" % j)
+            for h in range(PAIR):
+                nc.vector.tensor_scalar(
+                    out=unit_rows[:, h, :],
+                    in0=enriched[j, RIGHT][:, h, :],
+                    scalar1=inv_norm[j][:, h : h + 1],
                     scalar2=1.0,
                     op0=ALU.mult,
                     op1=ALU.mult,
                 )
-            enriched[2 * j, UNIT] = unit_rows
-            store(2 * j, 2, UNIT)
+            store(j, UNIT)
 
-        V = nc.vector.tensor_copy
+        def feature_unit(j, b):
+            return [(j, b, c) for c in range(0, GROUPS, WIDTH)]
 
-        def pair(j, b):
-            return (2 * j, 2, b, 0), (2 * j, 2, b, 2)
-
-        def quad(first, b, c):
-            return (first, 4, b, c), (first, 4, b, c + 1)
+        left = [feature_unit(j, LEFT) for j in range(PAIRS)]
+        head = [feature_unit(j, H0) for j in range(PAIRS)]
+        right = [feature_unit(j, RIGHT) for j in range(PAIRS)]
+        token = [[(PAIR * j + h,) for h in range(PAIR)] for j in range(PAIRS)]
 
         def multiply(shares):
             for share in shares:
@@ -408,128 +367,140 @@ def tile_avey_pa_kernel(tc, x, g, W1, b1, out_0, out_1, out_2):
             for share in shares:
                 finish(share)
 
-        keep_clock(3)
-        x_square(0)
+        def end_around(unit, step, *args):
+            end(unit[:1])
+            step(*args)
+            end(unit[1:])
+
+
+        for _ in range(3):
+            keep_clock(zeros[:])
+        x_sum(0)
         x_rstd(0, slice(0, 1))
-        x_square(1, "V")
-        x_rstd(0, slice(1, 2))
+        x_sum(1, "V")
+        x_rstd(0, slice(1, PAIR))
         spread(GAIN_ROW, gain)
         turned_bias = turn_bias()
         spread_b1 = psum_acc.tile([P, BANK], BF16, tag="acc", name="acc")
         spread(H1, spread_b1)
         x_stats(1)
         x_norm(0)
-        V(out=bias[:], in_=turned_bias[:, :, 0:BANKS])
+        nc.vector.tensor_copy(out=bias[:], in_=turned_bias[:, :, 0:BANKS])
         x_turn(0)
-        keep_clock(2)
+        for _ in range(2):
+            keep_clock(zeros[:])
         x_copy(0)
-        keep_clock(2, x_grouped[0][:].rearrange("p h r t -> p (h r t)")[:, 0:BANK])
-        w_group(LEFT, V)
+        for _ in range(2):
+            keep_clock(x_grouped[0][:, 0:BANK])
+        w_group(LEFT)
         x_stats(2)
         x_norm(1)
         x_turn(1)
-        keep_clock(1, zeros[:, 0 : 2 * P])
+        keep_clock(zeros[:, 0 : BANK // 2])
         x_quantise(0)
         w_quantise(LEFT)
         w_group_gpsimd(H0)
         x_stats(3)
         x_copy(1)
-        l = [pair(j, LEFT) for j in range(PAIRS)]
-        h = [pair(j, H0) for j in range(PAIRS)]
-        r = [pair(j, RIGHT) for j in range(PAIRS)]
-        t = [((2 * j,), (2 * j + 1,)) for j in range(PAIRS)]
-        multiply(l[0])
+
+        multiply(left[0])
         x_norm(2)
         x_turn(2)
-        keep_clock(1)
-        read(l[0], "S")
+        keep_clock(zeros[:])
+        read(left[0], "S")
         x_norm(3)
-        V(out=token_bias[:], in_=spread_b1[:])
+        nc.vector.tensor_copy(out=token_bias[:], in_=spread_b1[:])
         x_quantise(1)
         w_quantise(H0)
         x_copy(2)
-        end(l[0][:1])
-        keep_clock(1)
-        end(l[0][1:])
-        store(0, 2, LEFT)
-        multiply(l[1])
-        multiply(h[0])
+        end(left[0][:1])
+        keep_clock(zeros[:])
+        end(left[0][1:])
+        store(0, LEFT)
+        multiply(left[1])
+        multiply(head[0])
         x_quantise(2)
         w_group_gpsimd(H1)
-        read(l[1])
+        read(left[1])
         x_turn(3)
-        read(h[0][:1])
-        read(h[0][1:], "S")
+        read(head[0][:1])
+        read(head[0][1:], "S")
         x_copy(3)
-        multiply(l[2][:1])
-        end(l[1][:1])
-        multiply(l[2][1:])
-        end(l[1][1:])
-        store(2, 2, LEFT)
-        read(l[2])
-        end(h[0])
-        store(0, 2, H0)
-        multiply(h[1])
+        multiply(left[2][:1])
+        end(left[1][:1])
+        multiply(left[2][1:])
+        end(left[1][1:])
+        store(1, LEFT)
+        read(left[2])
+        end(head[0])
+        store(0, H0)
+        multiply(head[1])
         x_quantise(3)
         w_quantise(H1)
         w_group_gpsimd(RIGHT)
-        multiply(l[3])
-        end(l[2])
-        store(4, 2, LEFT)
-        read(h[1])
-        read(l[3])
-        multiply(t[0])
-        end(h[1])
-        store(2, 2, H0)
-        multiply(h[2])
-        read(t[0])
-        end(t[0])
-        end(l[3])
-        store(6, 2, LEFT)
+        multiply(left[3])
+        end(left[2])
+        store(2, LEFT)
+        read(head[1])
+        read(left[3])
+        multiply(token[0])
+        end(head[1])
+        store(1, H0)
+        multiply(head[2])
+        read(token[0])
+        end(token[0])
+        end(left[3])
+        store(3, LEFT)
         w_quantise(RIGHT)
-        read(h[2])
-        multiply(r[0])
-        multiply(h[3])
-        read(h[3][1:], "S")
-        end(h[2])
-        store(4, 2, H0)
-        read(r[0])
-        multiply(t[1])
-        end(r[0])
-        read(h[3][:1])
-        multiply(r[1])
-        read(t[1])
-        end(t[1])
-        end(h[3])
-        store(0, 2, H1)
-        store(6, 2, H0)
-        multiply(r[2])
+        read(head[2])
+
+        multiply(right[0])
+        multiply(head[3])
+        read(head[3][1:], "S")
+        end(head[2])
+        store(2, H0)
+        read(right[0])
+        multiply(token[1])
+        end(right[0])
+        read(head[3][:1])
+        multiply(right[1])
+        read(token[1])
+        end(token[1])
+        end(head[3])
+        store(0, H1)
+        store(3, H0)
+        multiply(right[2])
         right_sum(0, 0)
         right_sum(0, 1)
-        read(r[1])
-        multiply(r[3])
-        right_norm(0, r[1])
-        read(r[2])
-        multiply(t[2])
-        store(2, 2, H1)
+        read(right[1])
+        multiply(right[3])
+        end_around(right[1], right_floor, 0)
+        right_invert(0)
+        read(right[2])
+        multiply(token[2])
+        store(1, H1)
         right_sum(1, 0)
         right_sum(1, 1)
-        right_norm(1, r[2])
-        read(r[3])
-        multiply(t[3])
+        end_around(right[2], right_floor, 1)
+        right_invert(1)
+        read(right[3])
+        multiply(token[3])
+        end(right[3])
         right_sum(2, 0)
         right_sum(2, 1)
-        read(t[2])
-        right_scale(0, nc.vector)
-        right_norm(2, r[3])
-        end(t[2])
-        store(4, 2, H1)
-        right_sum(3, 0)
-        read(t[3])
-        right_scale(1, nc.vector)
-        end(t[3])
-        store(6, 2, H1)
-        right_sum(3, 1, "V")
-        right_norm(3)
-        right_scale(2, nc.vector)
-        right_scale(3, nc.vector)
+        right_floor(2)
+        right_invert(2)
+        right_sum(3, 1)
+        read(token[2])
+        right_store(0)
+        end(token[2])
+        store(2, H1)
+        read(token[3])
+        right_store(1)
+        end(token[3])
+        store(3, H1)
+        right_sum(3, 0, "V")
+        right_floor(3)
+        right_invert(3)
+        right_store(2)
+        right_store(3)

from contextlib import ExitStack

import concourse.masks as masks
import concourse.mybir as mybir

F32 = mybir.dt.float32
BF16 = mybir.dt.bfloat16
U32 = mybir.dt.uint32
U8 = mybir.dt.uint8
FP8X4 = mybir.dt.float8_e4m3fn_x4
ACT = mybir.ActivationFunctionType
ALU = mybir.AluOpType

P = 128
PACK = 4
MX_ALIGN = 64
TOKENS = 1024
D = 512
HEAD = 1024
HALF = 512
E = HEAD + HALF + HALF
BANK = 512
BANKS = E // BANK
GROUPS = BANK // P
TOK_TILES = TOKENS // P
PAIR = 2
PAIRS = TOK_TILES // PAIR
WIDTH = BANK // (PAIR * P)
GPSIMD_TOKENS = TOK_TILES // 2
GAIN_ROW = BANKS
FLT_MAX = 3.4028234663852886e38
EPS_RMS = 1e-6
EPS_NORM = 1e-12
EPS_NORM_SQUARED = EPS_NORM * EPS_NORM

FLOPS = 2 * TOKENS * D * E


def tile_avey_pa_kernel(tc, x, g, W1, b1, out_0, out_1, out_2):
    nc = tc.nc

    def token_rows(tensor):
        return tensor.flatten_outer_dims().rearrange("(p i) k -> p i k", i=TOK_TILES)

    x_rows = token_rows(x)
    w_rows = W1.rearrange("(p t) f -> p t f", t=PACK)

    H0, H1, LEFT, RIGHT = range(BANKS)
    UNIT = BANKS
    head_rows = token_rows(out_0)
    outputs = {
        H0: head_rows[:, :, 0:BANK],
        H1: head_rows[:, :, BANK:HEAD],
        LEFT: token_rows(out_1),
        UNIT: token_rows(out_2),
    }

    with ExitStack() as ctx:
        keep = ctx.enter_context(tc.tile_pool(name="keep", bufs=1))
        stage = ctx.enter_context(tc.tile_pool(name="stage", bufs=3))
        flip = ctx.enter_context(tc.tile_pool(name="flip", bufs=6))
        tokens = ctx.enter_context(tc.tile_pool(name="tokens", bufs=6))
        psum_gain = ctx.enter_context(tc.psum_pool(name="psum_gain", bufs=1))
        psum_turn = ctx.enter_context(tc.psum_pool(name="psum_turn", bufs=3))
        psum_acc = ctx.enter_context(tc.psum_pool(name="psum_acc", bufs=4))
        ctx.enter_context(tc.manual_schedule())

        x_first = [keep.tile([P, 1, D], BF16, name="x_first%d" % i) for i in range(PAIR)]
        x_pairs = [keep.tile([P, PAIR, D], BF16, name="x_pair%d" % j) for j in range(1, PAIRS)]
        x_sb = [tile[:, 0, :] for tile in x_first] + [tile[:, i, :] for tile in x_pairs for i in range(PAIR)]
        w_raw = [keep.tile([P, PACK, BANK], BF16, name="w_raw%d" % b) for b in range(BANKS)]

        def load_x(j):
            nc.sync.dma_start(out=x_pairs[j - 1][:], in_=x_rows[:, PAIR * j : PAIR * (j + 1), :])

        def load_w(b):
            nc.sync.dma_start(out=w_raw[b][:], in_=w_rows[:, :, b * BANK : (b + 1) * BANK])

        consts = keep.tile([P, BANK], BF16)
        nc.vector.memset(consts[:], 0.0)
        zeros = keep.tile([P, BANK], BF16)
        nc.vector.memset(zeros[:], 0.0)
        warm = keep.tile([P, 1], F32)
        nc.vector.memset(warm[:], 1.0)
        nc.scalar.activation(out=warm[:], in_=warm[:], func=ACT.Abs_reciprocal_sqrt)

        for i in range(PAIR):
            nc.sync.dma_start(out=x_first[i][:], in_=x_rows[:, i : i + 1, :])
        nc.sync.dma_start(out=consts[GAIN_ROW : GAIN_ROW + 1, :], in_=g.unsqueeze(0))
        nc.sync.dma_start(out=consts[0:BANKS, :], in_=b1.rearrange("(r c) -> r c", c=BANK))
        load_x(1)
        load_w(LEFT)
        load_x(2)
        load_w(H0)
        load_x(3)
        load_w(H1)
        load_w(RIGHT)

        ident = keep.tile([P, P], BF16)
        masks.make_identity(nc, ident[:])
        ident_f32 = keep.tile([P, P], F32)
        masks.make_identity(nc, ident_f32[:])

        gain = psum_gain.tile([P, D], BF16, tag="gain")
        bias = keep.tile([P, GROUPS, BANKS], F32)
        token_bias = keep.tile([P, BANK], BF16)

        def spread(row, acc):
            nc.tensor.matmul(
                out=acc[:],
                lhsT=ident[:, row : row + 1].to_broadcast([P, P]),
                rhs=consts[:],
                start=True,
                stop=True,
            )

        def turn_bias():
            turned = psum_turn.tile([P, GROUPS, P], BF16, tag="turn", name="turn")
            for c in range(GROUPS):
                nc.tensor.transpose(turned[:, c, :], consts[:, c * P : (c + 1) * P], ident[:])
            return turned

        idle = psum_acc.tile([P, BANK], F32, tag="acc", name="idle")

        def keep_clock(operand):
            nc.tensor.matmul(out=idle[:, 0 : operand.shape[1]], lhsT=ident[:], rhs=operand, start=True, stop=True)

        def mx_tile(shape, dtype, name):
            return keep.tile(shape, dtype, align_bytes=MX_ALIGN, name=name)

        x_grouped = [mx_tile([P, PAIR * P * PACK], BF16, "x_grouped%d" % j) for j in range(PAIRS)]
        x_codes = [mx_tile([P, PAIR * P], U32, "x_codes%d" % j) for j in range(PAIRS)]
        x_scales = [mx_tile([P, PAIR * P], U8, "x_scales%d" % j) for j in range(PAIRS)]
        w_grouped = [mx_tile([P, BANK, PACK], BF16, "w_grouped%d" % b) for b in range(BANKS)]
        w_codes = [mx_tile([P, BANK], U32, "w_codes%d" % b) for b in range(BANKS)]
        w_scales = [mx_tile([P, BANK], U8, "w_scales%d" % b) for b in range(BANKS)]
        square_sums = [keep.tile([P, PAIR], F32, name="square_sums%d" % j) for j in range(PAIRS)]
        rstd = [keep.tile([P, PAIR], F32, name="rstd%d" % j) for j in range(PAIRS)]

        def sum_squares(engine, rows, total):
            unread = stage.tile([P, BANK], BF16, name="unread" + engine)
            if engine == "S":
                nc.scalar.activation(out=unread[:], in_=rows, func=ACT.Square, accum_out=total)
            else:
                nc.vector.scalar_tensor_tensor(
                    out=unread[:], in0=rows, scalar=1.0, in1=rows, op0=ALU.mult, op1=ALU.mult, accum_out=total
                )

        def x_sum(i, engine="S"):
            j, h = divmod(i, PAIR)
            sum_squares(engine, x_sb[i], square_sums[j][:, h : h + 1])

        def x_rstd(j, here=slice(0, PAIR)):
            nc.scalar.activation(
                out=rstd[j][:, here],
                in_=square_sums[j][:, here],
                func=ACT.Abs_reciprocal_sqrt,
                bias=EPS_RMS,
                scale=1.0 / D,
            )

        def x_stats(j):
            for h in range(PAIR):
                x_sum(PAIR * j + h)
            x_rstd(j)

        normed = {}
        turned_x = {}

        def x_norm(j):
            normed[j] = xn = stage.tile([P, PAIR, D], BF16, name="xn")
            for h in range(PAIR):
                nc.vector.scalar_tensor_tensor(
                    out=xn[:, h, :],
                    in0=x_sb[PAIR * j + h],
                    scalar=rstd[j][:, h : h + 1],
                    in1=gain[:],
                    op0=ALU.mult,
                    op1=ALU.mult,
                )

        def x_turn(j):
            words = normed[j][:].bitcast(F32)
            turned_x[j] = turned = psum_turn.tile([P, PAIR, PACK // 2, P], F32, tag="turn", name="turn")
            for h in range(PAIR):
                for u in range(PACK // 2):
                    nc.tensor.transpose(turned[:, h, u, :], words[:, h, u :: PACK // 2], ident_f32[:])

        def x_copy(j):
            nc.scalar.copy(
                out=x_grouped[j][:].bitcast(F32),
                in_=turned_x[j][:].rearrange("p h u r -> p h r u"),
            )

        def x_quantise(j):
            nc.vector.quantize_mx(out=x_codes[j][:].bitcast(FP8X4), scales=x_scales[j][:], in_=x_grouped[j][:])

        def w_group(b):
            nc.vector.tensor_copy(
                out=w_grouped[b][:].rearrange("p (c i) t -> p c t i", i=PACK),
                in_=w_raw[b][:].rearrange("p t (c i) -> p c t i", i=PACK),
            )

        def w_group_gpsimd(b):
            go = keep.tile([P, 1], F32, name="go%d" % b)
            nc.vector.memset(go[:], 1.0)
            for half in range(2):
                here = slice(half * BANK // 2, (half + 1) * BANK // 2)
                nc.gpsimd.tensor_scalar(
                    out=w_grouped[b][:, here, :],
                    in0=w_raw[b][:, :, here].rearrange("p t f -> p f t"),
                    scalar1=go[:, 0:1],
                    scalar2=1.0,
                    op0=ALU.mult,
                    op1=ALU.mult,
                )

        def w_quantise(b):
            nc.vector.quantize_mx(
                out=w_codes[b][:].bitcast(FP8X4),
                scales=w_scales[b][:],
                in_=w_grouped[b][:].rearrange("p f t -> p (f t)"),
            )

        enriched = {}
        products = {}
        reads = {}
        turns = []

        def matmul(share):
            products[share] = acc = psum_acc.tile([P, BANK], F32, tag="acc", name="acc")
            if len(share) == 1:
                j, h = divmod(share[0], PAIR)
                toks = slice(h * P, (h + 1) * P)
                nc.tensor.matmul_mx(
                    out=acc[:],
                    lhsT=x_codes[j][:, toks].bitcast(FP8X4),
                    lhsT_scale=x_scales[j][:, toks],
                    rhs=w_codes[H1][:].bitcast(FP8X4),
                    rhs_scale=w_scales[H1][:],
                    start=True,
                    stop=True,
                )
                return
            j, b, c = share
            for n in range(WIDTH):
                feats = slice((c + n) * P, (c + n + 1) * P)
                nc.tensor.matmul_mx(
                    out=acc[:, n * PAIR * P : (n + 1) * PAIR * P],
                    lhsT=w_codes[b][:, feats].bitcast(FP8X4),
                    lhsT_scale=w_scales[b][:, feats],
                    rhs=x_codes[j][:].bitcast(FP8X4),
                    rhs_scale=x_scales[j][:],
                    start=True,
                    stop=True,
                )

        def drain(share, engine):
            acc = products[share]
            if len(share) == 1:
                reads[share] = mid = tokens.tile([P, BANK], F32, name="mid")
                nc.vector.tensor_tensor(out=mid[:], in0=acc[:], in1=token_bias[:], op=ALU.add)
                return
            j, b, c = share
            reads[share] = mid = flip.tile([P, BANK], F32, name="mid_flip")
            for n in range(WIDTH):
                part = slice(n * PAIR * P, (n + 1) * PAIR * P)
                b1_column = bias[:, c + n, b : b + 1]
                if engine == "S":
                    nc.scalar.activation(out=mid[:, part], in_=acc[:, part], func=ACT.Relu, bias=b1_column)
                else:
                    nc.vector.tensor_scalar(
                        out=mid[:, part],
                        in0=acc[:, part],
                        scalar1=b1_column,
                        scalar2=0.0,
                        op0=ALU.add,
                        op1=ALU.max,
                    )

        def finish_tokens(i):
            mid = reads[(i,)]
            j, h = divmod(i, PAIR)
            if h == 0:
                enriched[j, H1] = keep.tile([P, PAIR, BANK], F32, name="enriched_h1_%d" % j)
            result = enriched[j, H1][:, h, :]
            if i >= GPSIMD_TOKENS:
                nc.vector.scalar_tensor_tensor(
                    out=result, in0=mid[:], scalar=0.0, in1=mid[:], op0=ALU.max, op1=ALU.mult
                )
                return
            above = tokens.tile([P, BANK], F32, name="above")
            nc.gpsimd.tensor_scalar(
                out=above[:], in0=mid[:], scalar1=FLT_MAX, scalar2=0.0, op0=ALU.min, op1=ALU.max
            )
            nc.gpsimd.tensor_tensor(out=result, in0=above[:], in1=above[:], op=ALU.mult)

        def finish(share):
            if len(share) == 1:
                finish_tokens(share[0])
                return
            mid = reads[share]
            j, b, c = share
            if c == 0:
                enriched[j, b] = keep.tile([P, PAIR, BANK], F32, name="enriched%d_%d" % (b, j))
            pool, tag = (psum_gain, "gain") if len(turns) % 4 == 3 else (psum_turn, "turn")
            turns.append(share)
            turned = pool.tile([P, PAIR, WIDTH, P], F32, tag=tag, name="turn")
            for n in range(WIDTH):
                for h in range(PAIR):
                    toks = slice((n * PAIR + h) * P, (n * PAIR + h + 1) * P)
                    nc.tensor.transpose(turned[:, h, n, :], mid[:, toks], ident_f32[:])
            nc.scalar.activation(
                out=enriched[j, b][:, :, c * P : (c + WIDTH) * P],
                in_=turned[:].rearrange("p h n r -> p h (n r)"),
                func=ACT.Square,
            )

        def store(j, b):
            nc.sync.dma_start(out=outputs[b][:, PAIR * j : PAIR * (j + 1), :], in_=enriched[j, b][:])

        norm2 = [keep.tile([P, PAIR], F32, name="norm2_%d" % j) for j in range(PAIRS)]
        over = [keep.tile([P, PAIR], F32, name="over%d" % j) for j in range(PAIRS)]
        inv_norm = [keep.tile([P, PAIR], F32, name="inv_norm%d" % j) for j in range(PAIRS)]

        def right_sum(j, h, engine="S"):
            sum_squares(engine, enriched[j, RIGHT][:, h, :], norm2[j][:, h : h + 1])

        def right_floor(j):
            nc.scalar.activation(out=over[j][:], in_=norm2[j][:], func=ACT.Relu, bias=-EPS_NORM_SQUARED)

        def right_invert(j):
            nc.scalar.activation(
                out=inv_norm[j][:], in_=over[j][:], func=ACT.Abs_reciprocal_sqrt, bias=EPS_NORM_SQUARED
            )

        def right_store(j):
            enriched[j, UNIT] = unit_rows = keep.tile([P, PAIR, HALF], F32, name="unit_rows%d" % j)
            for h in range(PAIR):
                nc.vector.tensor_scalar(
                    out=unit_rows[:, h, :],
                    in0=enriched[j, RIGHT][:, h, :],
                    scalar1=inv_norm[j][:, h : h + 1],
                    scalar2=1.0,
                    op0=ALU.mult,
                    op1=ALU.mult,
                )
            store(j, UNIT)

        def feature_unit(j, b):
            return [(j, b, c) for c in range(0, GROUPS, WIDTH)]

        left = [feature_unit(j, LEFT) for j in range(PAIRS)]
        head = [feature_unit(j, H0) for j in range(PAIRS)]
        right = [feature_unit(j, RIGHT) for j in range(PAIRS)]
        token = [[(PAIR * j + h,) for h in range(PAIR)] for j in range(PAIRS)]

        def multiply(shares):
            for share in shares:
                matmul(share)

        def read(shares, engine="V"):
            for share in shares:
                drain(share, engine)

        def end(shares):
            for share in shares:
                finish(share)

        def end_around(unit, step, *args):
            end(unit[:1])
            step(*args)
            end(unit[1:])


        for _ in range(3):
            keep_clock(zeros[:])
        x_sum(0)
        x_rstd(0, slice(0, 1))
        x_sum(1, "V")
        x_rstd(0, slice(1, PAIR))
        spread(GAIN_ROW, gain)
        turned_bias = turn_bias()
        spread_b1 = psum_acc.tile([P, BANK], BF16, tag="acc", name="acc")
        spread(H1, spread_b1)
        x_stats(1)
        x_norm(0)
        nc.vector.tensor_copy(out=bias[:], in_=turned_bias[:, :, 0:BANKS])
        x_turn(0)
        for _ in range(2):
            keep_clock(zeros[:])
        x_copy(0)
        for _ in range(2):
            keep_clock(x_grouped[0][:, 0:BANK])
        w_group(LEFT)
        x_stats(2)
        x_norm(1)
        x_turn(1)
        keep_clock(zeros[:, 0 : BANK // 2])
        x_quantise(0)
        w_quantise(LEFT)
        w_group_gpsimd(H0)
        x_stats(3)
        x_copy(1)

        multiply(left[0])
        x_norm(2)
        x_turn(2)
        keep_clock(zeros[:])
        read(left[0], "S")
        x_norm(3)
        nc.vector.tensor_copy(out=token_bias[:], in_=spread_b1[:])
        x_quantise(1)
        w_quantise(H0)
        x_copy(2)
        end(left[0][:1])
        keep_clock(zeros[:])
        end(left[0][1:])
        store(0, LEFT)
        multiply(left[1])
        multiply(head[0])
        x_quantise(2)
        w_group_gpsimd(H1)
        read(left[1])
        x_turn(3)
        read(head[0][:1])
        read(head[0][1:], "S")
        x_copy(3)
        multiply(left[2][:1])
        end(left[1][:1])
        multiply(left[2][1:])
        end(left[1][1:])
        store(1, LEFT)
        read(left[2])
        end(head[0])
        store(0, H0)
        multiply(head[1])
        x_quantise(3)
        w_quantise(H1)
        w_group_gpsimd(RIGHT)
        multiply(left[3])
        end(left[2])
        store(2, LEFT)
        read(head[1])
        read(left[3])
        multiply(token[0])
        end(head[1])
        store(1, H0)
        multiply(head[2])
        read(token[0])
        end(token[0])
        end(left[3])
        store(3, LEFT)
        w_quantise(RIGHT)
        read(head[2])

        multiply(right[0])
        multiply(head[3])
        read(head[3][1:], "S")
        end(head[2])
        store(2, H0)
        read(right[0])
        multiply(token[1])
        end(right[0])
        read(head[3][:1])
        multiply(right[1])
        read(token[1])
        end(token[1])
        end(head[3])
        store(0, H1)
        store(3, H0)
        multiply(right[2])
        right_sum(0, 0)
        right_sum(0, 1)
        read(right[1])
        multiply(right[3])
        end_around(right[1], right_floor, 0)
        right_invert(0)
        read(right[2])
        multiply(token[2])
        store(1, H1)
        right_sum(1, 0)
        right_sum(1, 1)
        end_around(right[2], right_floor, 1)
        right_invert(1)
        read(right[3])
        multiply(token[3])
        end(right[3])
        right_sum(2, 0)
        right_sum(2, 1)
        right_floor(2)
        right_invert(2)
        right_sum(3, 1)
        read(token[2])
        right_store(0)
        end(token[2])
        store(2, H1)
        read(token[3])
        right_store(1)
        end(token[3])
        store(3, H1)
        right_sum(3, 0, "V")
        right_floor(3)
        right_invert(3)
        right_store(2)
        right_store(3)
